import numpy as np
import ml_dtypes


def mxq(x, axis, fmt="e4m3"):
    dtype, down = {"e4m3": (ml_dtypes.float8_e4m3fn, 7), "e5m2": (ml_dtypes.float8_e5m2, 14)}[fmt]
    v = np.moveaxis(np.asarray(x, np.float32).astype(ml_dtypes.bfloat16).astype(np.float64), axis, -1)
    blocks = v.reshape(v.shape[:-1] + (-1, 32))
    amax = np.abs(blocks).max(-1, keepdims=True)
    byte = np.maximum(np.where(amax > 0, np.frexp(amax)[1] - 1 + 127, 0) - down, 1)
    scale = np.exp2(byte - 127.0)
    codes = (blocks / scale).astype(np.float32).astype(dtype).astype(np.float64)
    return np.moveaxis((codes * scale).reshape(v.shape), -1, axis)


WIDE = False


def mx_kscale(k):
    if not WIDE:
        return np.ones(k)
    levels = np.array([10, -10, 5, -5, 0])
    if k % 512:
        return np.exp2(np.random.permutation(np.resize(levels, k // 32))).repeat(32)
    a = np.empty((k // 512, 16))
    for p in range(k // 512):
        a[p, :8] = np.random.permutation(np.resize(levels, 8))
        for g in range(8):
            far = levels[np.abs(levels - a[p, g]) >= 10]
            a[p, g + 8] = far[np.random.randint(len(far))]
    return np.exp2(a.ravel()).repeat(32)


BF16 = ml_dtypes.bfloat16


def bf(x):
    return np.asarray(x, np.float32).astype(BF16)


def f64(x):
    return np.asarray(x).astype(np.float64)


T, H, NQ, NKV, HD = 8192, 1024, 2, 1, 64
RD = HD // 2
QS, KS = NQ * HD, NKV * HD
OUT = QS + 2 * KS


def extract_rope(x):
    r = x[..., :RD]
    r = r.reshape(*r.shape[:-1], RD // 2, 2)
    return np.swapaxes(r, -2, -1).reshape(*x.shape[:-1], RD)


def fill_rope(x, rope):
    r = rope.reshape(*rope.shape[:-1], 2, RD // 2)
    r = np.swapaxes(r, -2, -1).reshape(*rope.shape)
    return np.concatenate([r, x[..., RD:]], axis=-1)


def rotate_half(x):
    half = x.shape[-1] // 2
    return np.concatenate([-x[..., half:], x[..., :half]], axis=-1)


def setup_inputs():
    s = mx_kscale(H)
    ang = np.random.uniform(0.0, 2.0 * np.pi, (T, RD))
    return {'hidden_states': bf(np.random.standard_normal((T, H)) * s),
            'cos': bf(np.cos(ang)), 'sin': bf(np.sin(ang)),
            'W_qkv': bf(np.random.standard_normal((H, OUT)) / np.sqrt(H) / s[:, None]),
            'b_qkv': bf(np.random.standard_normal(OUT) * 0.3)}


def reference(hidden_states, cos, sin, W_qkv, b_qkv):
    qkv = (mxq(f64(hidden_states), 1, 'e4m3') @ mxq(f64(W_qkv), 0, 'e4m3')) + f64(b_qkv)
    q = qkv[:, :QS].reshape(T, NQ, HD)
    k = qkv[:, QS:QS + KS].reshape(T, NKV, HD)
    v = qkv[:, QS + KS:].reshape(T, NKV, HD)
    cos_b = f64(cos)[:, None, :]
    sin_b = f64(sin)[:, None, :]
    q_r = extract_rope(q)
    k_r = extract_rope(k)
    q_r = q_r * cos_b + rotate_half(q_r) * sin_b
    k_r = k_r * cos_b + rotate_half(k_r) * sin_b
    q = fill_rope(q, q_r)
    k = fill_rope(k, k_r)
    return q, k, v

@@ -1,0 +1,316 @@
+from contextlib import ExitStack
+
+import concourse.mybir as mybir
+from concourse.masks import make_identity
+
+F32 = mybir.dt.float32
+BF16 = mybir.dt.bfloat16
+U32 = mybir.dt.uint32
+U8 = mybir.dt.uint8
+FP8X4 = mybir.dt.float8_e4m3fn_x4
+ALU = mybir.AluOpType
+ACT = mybir.ActivationFunctionType
+
+P = 128
+T, H, OUT = 8192, 1024, 256
+NT = T // P
+FLOPS = 2 * T * H * OUT
+
+ROUNDS = [2, 2] + [4] * 14 + [2, 2]
+GROUPS = [[0, 1]] + [[2 + 2 * g, 3 + 2 * g] for g in range(7)] + [[16], [17]]
+HEAD = ["x0", "x1", "x2", "x3", "sc", "x4", "x5", "x6", "x7"]
+XB = 8
+RMAX = 4
+GMAX = 8
+KU_ON_SCALAR = True
+
+
+def tile_selfattention_pa_t_kernel(tc, hidden_states, cos, sin, W_qkv, b_qkv, out_0, out_1, out_2):
+    nc = tc.nc
+    nr = len(ROUNDS)
+    first = [sum(ROUNDS[:r]) for r in range(nr)]
+    group_of = {}
+    for g, rs in enumerate(GROUPS):
+        for r in rs:
+            group_of[r] = g
+    x_v = hidden_states.rearrange("(p i) k -> p i k", i=NT)
+    q_v = out_0.rearrange("(p i) h d -> p i (h d)", i=NT)
+    k_v = out_1.rearrange("(p i) h d -> p i (h d)", i=NT)
+    v_v = out_2.rearrange("(p i) h d -> p i (h d)", i=NT)
+
+    with ExitStack() as ctx:
+        ctx.enter_context(tc.manual_schedule())
+        const = ctx.enter_context(tc.tile_pool(name="const", bufs=1))
+        xpool = ctx.enter_context(tc.tile_pool(name="xpool", bufs=XB))
+        gpool = ctx.enter_context(tc.tile_pool(name="gpool", bufs=4))
+        opool = ctx.enter_context(tc.tile_pool(name="opool", bufs=4))
+        spool = ctx.enter_context(tc.tile_pool(name="spool", bufs=2))
+        ps_x = ctx.enter_context(tc.psum_pool(name="ps_x", bufs=4))
+        ps_n = ctx.enter_context(tc.psum_pool(name="ps_n", bufs=1))
+        ps_t = ctx.enter_context(tc.psum_pool(name="ps_t", bufs=1))
+        ps_b = ctx.enter_context(tc.psum_pool(name="ps_b", bufs=2))
+
+        x_t, xt_t, grp_t, codes_t, scl_t, pn_t, pt_t, xr_t, pb_t, o_t, t1_t, t2_t = {}, {}, {}, {}, {}, {}, {}, {}, {}, {}, {}, {}
+
+        def gsize(g):
+            return sum([ROUNDS[j] for j in GROUPS[g]])
+
+        def load(r):
+            nt = ROUNDS[r]
+            xc = xpool.tile([P, RMAX * H], BF16)
+            nc.sync.dma_start(
+                out=xc[:, 0 : nt * H].rearrange("p (n k) -> p n k", k=H),
+                in_=x_v[:, first[r] : first[r] + nt, :],
+            )
+            x_t[r] = xc
+
+        def transp(r):
+            xw = x_t[r][:].bitcast(F32)
+            xt_t[r] = []
+            for a in range(ROUNDS[r]):
+                xt = ps_x.tile([P, 4, P], F32)
+                for b in range(4):
+                    w0 = a * 512 + (b // 2) * 256 + b % 2
+                    nc.tensor.transpose(xt[:, b, :], xw[:, w0 : w0 + 255 : 2], ident[:])
+                xt_t[r].append(xt)
+
+        def copyout(r):
+            nt = ROUNDS[r]
+            grp = gpool.tile([P, RMAX * H], BF16, align_bytes=64)
+            gw = grp[:].bitcast(F32)[:, 0 : nt * 512].rearrange("p (g a m u) -> p g a m u", g=2, a=nt, u=2)
+            for a in range(nt):
+                nc.scalar.copy(out=gw[:, :, a], in_=xt_t[r][a][:].rearrange("p (g u) m -> p g m u", u=2))
+            grp_t[r] = grp
+
+        def quant(r):
+            nt = ROUNDS[r]
+            codes = gpool.tile([P, RMAX * 256], U32, align_bytes=64)
+            scl = gpool.tile([P, RMAX * 256], U8, align_bytes=64)
+            nc.vector.quantize_mx(
+                out=codes[:, 0 : nt * 256].bitcast(FP8X4),
+                scales=scl[:, 0 : nt * 256],
+                in_=grp_t[r][:, 0 : nt * H],
+            )
+            codes_t[r] = codes
+            scl_t[r] = scl
+
+        def mx(r):
+            nt = ROUNDS[r]
+            w = nt * P
+            pt = ps_t.tile([P, RMAX * P], F32)
+            for g in range(2):
+                nc.tensor.matmul_mx(
+                    out=pt[:, 0:w],
+                    lhsT=w_codes[g][:, 0:P].bitcast(FP8X4),
+                    lhsT_scale=w_scl[g][:, 0:P],
+                    rhs=codes_t[r][:, g * w : (g + 1) * w].bitcast(FP8X4),
+                    rhs_scale=scl_t[r][:, g * w : (g + 1) * w],
+                    start=(g == 0),
+                    stop=(g == 1),
+                )
+            pn = ps_n.tile([P, RMAX, P], F32)
+            for a in range(nt):
+                for g in range(2):
+                    s0 = g * w + a * P
+                    nc.tensor.matmul_mx(
+                        out=pn[:, a, :],
+                        lhsT=codes_t[r][:, s0 : s0 + P].bitcast(FP8X4),
+                        lhsT_scale=scl_t[r][:, s0 : s0 + P],
+                        rhs=w_codes[g][:, P:OUT].bitcast(FP8X4),
+                        rhs_scale=w_scl[g][:, P:OUT],
+                        start=(g == 0),
+                        stop=(g == 1),
+                    )
+            pt_t[r] = pt
+            pn_t[r] = pn
+
+        def evac(r):
+            w = ROUNDS[r] * P
+            xr = spool.tile([P, RMAX * P], F32)
+            nc.scalar.activation(out=xr[:, 0:w], in_=pt_t[r][:, 0:w], func=ACT.Identity, bias=b_col[:, 0:1], scale=1.0)
+            xr_t[r] = xr
+
+        def tback(r):
+            pb = ps_b.tile([P, RMAX, P], F32)
+            for a in range(ROUNDS[r]):
+                nc.tensor.transpose(pb[:, a, :], xr_t[r][:, a * P : (a + 1) * P], ident[:])
+            pb_t[r] = pb
+
+        def bias_add(r):
+            g = group_of[r]
+            nt = ROUNDS[r]
+            gn = gsize(g)
+            n0 = first[r] - first[GROUPS[g][0]]
+            if r == GROUPS[g][0]:
+                o = opool.tile([P, GMAX * OUT], F32)
+                o_t[g] = o
+            o = o_t[g]
+            nc.vector.tensor_tensor(
+                out=o[:, 0 : gn * P].rearrange("p (n h d) -> p n h d", h=2, d=64)[:, n0 : n0 + nt, :, 32:64],
+                in0=pn_t[r][:, 0:nt, 0:64].rearrange("p n (h c) -> p n h c", h=2),
+                in1=bb_nr[:, 0:64].rearrange("p (h c) -> p h c", h=2).unsqueeze(1).to_broadcast([P, nt, 2, 32]),
+                op=ALU.add,
+            )
+            nc.vector.tensor_tensor(
+                out=o[:, gn * 192 : gn * OUT].rearrange("p (n c) -> p n c", c=64)[:, n0 : n0 + nt, :],
+                in0=pn_t[r][:, 0:nt, 64:P],
+                in1=bb_nr[:, 64:P].unsqueeze(1).to_broadcast([P, nt, 64]),
+                op=ALU.add,
+            )
+
+        def rope_mul(r):
+            g = group_of[r]
+            nt = ROUNDS[r]
+            gn = gsize(g)
+            i0 = first[r]
+            n0 = first[r] - first[GROUPS[g][0]]
+            if r == GROUPS[g][0]:
+                t1 = spool.tile([P, 3 * GMAX * 32], F32)
+                t2 = spool.tile([P, 3 * GMAX * 32], F32)
+                t1_t[g] = t1
+                t2_t[g] = t2
+            t1v = t1_t[g][:].rearrange("p (h n c) -> p n h c", h=3, c=32)[:, n0 : n0 + nt]
+            t2v = t2_t[g][:].rearrange("p (h n c) -> p n h c", h=3, c=32)[:, n0 : n0 + nt]
+            cosv = cos_sb[:].rearrange("p (i c) -> p i c", c=32)[:, i0 : i0 + nt, :]
+            sinv = sin_sb[:].rearrange("p (i c) -> p i c", c=32)[:, i0 : i0 + nt, :]
+            xv = pb_t[r][:, 0:nt, 0:96].rearrange("p n (h c) -> p n h c", h=3)
+            nc.vector.tensor_tensor(out=t1v, in0=xv, in1=cosv.unsqueeze(2).to_broadcast([P, nt, 3, 32]), op=ALU.mult)
+            for e in range(2):
+                lo, ot = 16 * e, 16 * (1 - e)
+                nc.vector.tensor_tensor(
+                    out=t2v[:, :, :, lo : lo + 16],
+                    in0=xv[:, :, :, ot : ot + 16],
+                    in1=sinv[:, :, lo : lo + 16].unsqueeze(2).to_broadcast([P, nt, 3, 16]),
+                    op=ALU.mult,
+                )
+            ku_out = o_t[g][:, gn * P : gn * 192].rearrange("p (n d) -> p n d", d=64)[:, n0 : n0 + nt, 32:64]
+            if KU_ON_SCALAR:
+                nc.scalar.copy(out=ku_out, in_=pb_t[r][:, 0:nt, 96:P])
+            else:
+                nc.vector.tensor_copy(out=ku_out, in_=pb_t[r][:, 0:nt, 96:P])
+
+        def rope_add(g):
+            gn = gsize(g)
+            o = o_t[g]
+            for h in range(3):
+                if h < 2:
+                    dst = o[:, 0 : gn * P].rearrange("p (n h d) -> p n h d", h=2, d=64)[:, :, h, 0:32]
+                else:
+                    dst = o[:, gn * P : gn * 192].rearrange("p (n d) -> p n d", d=64)[:, :, 0:32]
+                s0 = h * GMAX * 32
+                nc.vector.tensor_tensor(
+                    out=dst.rearrange("p n (j e) -> p n j e", e=2),
+                    in0=t1_t[g][:, s0 : s0 + gn * 32].rearrange("p (n e j) -> p n j e", e=2, j=16),
+                    in1=t2_t[g][:, s0 : s0 + gn * 32].rearrange("p (n e j) -> p n j e", e=2, j=16),
+                    op=ALU.add,
+                )
+
+        def store(g):
+            gn = gsize(g)
+            i0 = first[GROUPS[g][0]]
+            o = o_t[g]
+            nc.sync.dma_start(out=q_v[:, i0 : i0 + gn, :], in_=o[:, 0 : gn * P].rearrange("p (n c) -> p n c", c=P))
+            nc.sync.dma_start(
+                out=k_v[:, i0 : i0 + gn, :], in_=o[:, gn * P : gn * 192].rearrange("p (n c) -> p n c", c=64)
+            )
+            nc.sync.dma_start(
+                out=v_v[:, i0 : i0 + gn, :], in_=o[:, gn * 192 : gn * OUT].rearrange("p (n c) -> p n c", c=64)
+            )
+
+        ident = const.tile([P, P], F32)
+        make_identity(nc, ident[:])
+        b_row = const.tile([P, OUT], BF16)
+        nc.vector.memset(b_row[:], 0.0)
+        ones = const.tile([P, P], BF16)
+        nc.vector.memset(ones[:], 1.0)
+        warm = const.tile([P, 1], F32)
+        nc.scalar.activation(out=warm[:], in_=ones[:, 0:1], func=ACT.Identity, scale=1.0)
+
+        nc.sync.dma_start(out=b_row[0:1, :], in_=b_qkv.rearrange("(o c) -> o c", o=1))
+        w_raw = const.tile([P, 2 * 4 * OUT], BF16)
+        nc.sync.dma_start(
+            out=w_raw[:].rearrange("p (g f) -> p g f", g=2),
+            in_=W_qkv.rearrange("(g p t) c -> p g (t c)", g=2, t=4),
+        )
+        sin_sb = const.tile([P, NT * 32], BF16)
+        cos_sb = const.tile([P, NT * 32], BF16)
+        for item in HEAD:
+            if item[0] == "x":
+                load(int(item[1:]))
+            else:
+                nc.sync.dma_start(out=sin_sb[:], in_=sin.rearrange("(p i) c -> p (i c)", i=NT))
+                nc.sync.dma_start(out=cos_sb[:], in_=cos.rearrange("(p i) c -> p (i c)", i=NT))
+
+        sneg = sin_sb[:].rearrange("p (i e j) -> p i e j", e=2, j=16)[:, :, 0, :]
+        nc.gpsimd.tensor_scalar(out=sneg, in0=sneg, scalar1=-1.0, scalar2=0.0, op0=ALU.mult, op1=ALU.add)
+
+        pbias = ps_n.tile([P, RMAX, P], F32, tag="pn")
+        pb2 = pbias[:].rearrange("p a c -> p (a c)")[:, 0:OUT]
+        nc.tensor.matmul(out=pb2, lhsT=ones[:], rhs=b_row[:], start=True, stop=True)
+        pbv = pb2.rearrange("p (n m) -> p n m", n=4)
+        bb_rp = const.tile([P, P], F32)
+        bb_nr = const.tile([P, P], F32)
+        for e in range(2):
+            nc.scalar.copy(
+                out=bb_rp[:, 0:96].rearrange("p (h c) -> p h c", h=3)[:, :, 16 * e : 16 * e + 16], in_=pbv[:, 0:3, e:32:2]
+            )
+        nc.scalar.copy(out=bb_rp[:, 96:P], in_=pbv[:, 2, 32:64])
+        nc.scalar.copy(out=bb_nr[:, 0:64].rearrange("p (h c) -> p h c", h=2), in_=pbv[:, 0:2, 32:64])
+        nc.scalar.copy(out=bb_nr[:, 64:P], in_=pbv[:, 3, :])
+        b_col = const.tile([P, 1], F32)
+
+        def bias_column():
+            pbt = ps_b.tile([P, RMAX, P], F32, tag="pb")
+            nc.tensor.transpose(pbt[:, 0, :], bb_rp[:], ident[:])
+            nc.scalar.copy(out=b_col[:], in_=pbt[:, 0, 0:1])
+
+        w_codes, w_scl = [], []
+
+        def w_prep():
+            for g in range(2):
+                w_grp = const.tile([P, OUT * 4], BF16, name="w_grp%d" % g, align_bytes=64)
+                src = w_raw[:, g * 1024 : (g + 1) * 1024].rearrange("p (t n m) -> p n m t", t=4, n=4)
+                for e in range(2):
+                    nc.vector.tensor_copy(
+                        out=w_grp[:, 0 : 96 * 4].rearrange("p (h m t) -> p h m t", h=3, t=4)[:, :, 16 * e : 16 * e + 16, :],
+                        in_=src[:, 0:3, e:32:2, :],
+                    )
+                nc.vector.tensor_copy(
+                    out=w_grp[:, 96 * 4 : P * 4].rearrange("p (m t) -> p m t", t=4), in_=src[:, 2, 32:64, :]
+                )
+                nc.vector.tensor_copy(
+                    out=w_grp[:, P * 4 : 192 * 4].rearrange("p (h m t) -> p h m t", h=2, t=4), in_=src[:, 0:2, 32:64, :]
+                )
+                nc.vector.tensor_copy(
+                    out=w_grp[:, 192 * 4 : OUT * 4].rearrange("p (m t) -> p m t", t=4), in_=src[:, 3, :, :]
+                )
+                wc = const.tile([P, OUT], U32, name="w_codes%d" % g, align_bytes=64)
+                ws = const.tile([P, OUT], U8, name="w_scl%d" % g, align_bytes=64)
+                nc.vector.quantize_mx(out=wc[:].bitcast(FP8X4), scales=ws[:], in_=w_grp[:])
+                w_codes.append(wc)
+                w_scl.append(ws)
+
+        for p in range(-2, nr + 1):
+            if 0 <= p + 2 < nr:
+                transp(p + 2)
+                if p + 2 + XB < nr:
+                    load(p + 2 + XB)
+                copyout(p + 2)
+            if p == -1:
+                bias_column()
+                w_prep()
+            if 0 <= p + 1 < nr:
+                quant(p + 1)
+            if 0 <= p < nr:
+                bias_add(p)
+            if 0 <= p + 1 < nr:
+                mx(p + 1)
+                evac(p + 1)
+            if 0 <= p - 1 < nr:
+                rope_mul(p - 1)
+                g = group_of[p - 1]
+                if p - 1 == GROUPS[g][-1]:
+                    rope_add(g)
+                    store(g)
+            if 0 <= p < nr:
+                tback(p)

@@ -16,13 +16,11 @@ T, H, OUT = 8192, 1024, 256
 NT = T // P
 FLOPS = 2 * T * H * OUT
 
-ROUNDS = [2, 2] + [4] * 14 + [2, 2]
-GROUPS = [[0, 1]] + [[2 + 2 * g, 3 + 2 * g] for g in range(7)] + [[16], [17]]
-HEAD = ["x0", "x1", "x2", "x3", "sc", "x4", "x5", "x6", "x7"]
+ROUNDS = [1, 1, 2] + [4] * 14 + [2, 1, 1]
+GROUPS = [[0, 1, 2]] + [[3 + 2 * g, 4 + 2 * g] for g in range(7)] + [[17], [18], [19]]
 XB = 8
 RMAX = 4
 GMAX = 8
-KU_ON_SCALAR = True
 
 
 def tile_selfattention_pa_t_kernel(tc, hidden_states, cos, sin, W_qkv, b_qkv, out_0, out_1, out_2):
@@ -46,11 +44,9 @@ def tile_selfattention_pa_t_kernel(tc, hidden_states, cos, sin, W_qkv, b_qkv, ou
         opool = ctx.enter_context(tc.tile_pool(name="opool", bufs=4))
         spool = ctx.enter_context(tc.tile_pool(name="spool", bufs=2))
         ps_x = ctx.enter_context(tc.psum_pool(name="ps_x", bufs=4))
-        ps_n = ctx.enter_context(tc.psum_pool(name="ps_n", bufs=1))
-        ps_t = ctx.enter_context(tc.psum_pool(name="ps_t", bufs=1))
-        ps_b = ctx.enter_context(tc.psum_pool(name="ps_b", bufs=2))
+        ps_n = ctx.enter_context(tc.psum_pool(name="ps_n", bufs=4))
 
-        x_t, xt_t, grp_t, codes_t, scl_t, pn_t, pt_t, xr_t, pb_t, o_t, t1_t, t2_t = {}, {}, {}, {}, {}, {}, {}, {}, {}, {}, {}, {}
+        x_t, xt_t, grp_t, codes_t, scl_t, pn_t, o_t, t1_t, t2_t = {}, {}, {}, {}, {}, {}, {}, {}, {}
 
         def gsize(g):
             return sum([ROUNDS[j] for j in GROUPS[g]])
@@ -97,113 +93,101 @@ def tile_selfattention_pa_t_kernel(tc, hidden_states, cos, sin, W_qkv, b_qkv, ou
         def mx(r):
             nt = ROUNDS[r]
             w = nt * P
-            pt = ps_t.tile([P, RMAX * P], F32)
-            for g in range(2):
-                nc.tensor.matmul_mx(
-                    out=pt[:, 0:w],
-                    lhsT=w_codes[g][:, 0:P].bitcast(FP8X4),
-                    lhsT_scale=w_scl[g][:, 0:P],
-                    rhs=codes_t[r][:, g * w : (g + 1) * w].bitcast(FP8X4),
-                    rhs_scale=scl_t[r][:, g * w : (g + 1) * w],
-                    start=(g == 0),
-                    stop=(g == 1),
-                )
-            pn = ps_n.tile([P, RMAX, P], F32)
+            pn_t[r] = []
             for a in range(nt):
+                if a % 2 == 0:
+                    pn = ps_n.tile([P, 2, OUT], F32)
+                    pn_t[r].append(pn)
                 for g in range(2):
                     s0 = g * w + a * P
                     nc.tensor.matmul_mx(
-                        out=pn[:, a, :],
+                        out=pn[:, a % 2, :],
                         lhsT=codes_t[r][:, s0 : s0 + P].bitcast(FP8X4),
                         lhsT_scale=scl_t[r][:, s0 : s0 + P],
-                        rhs=w_codes[g][:, P:OUT].bitcast(FP8X4),
-                        rhs_scale=w_scl[g][:, P:OUT],
+                        rhs=w_codes[g][:].bitcast(FP8X4),
+                        rhs_scale=w_scl[g][:],
                         start=(g == 0),
                         stop=(g == 1),
                     )
-            pt_t[r] = pt
-            pn_t[r] = pn
-
-        def evac(r):
-            w = ROUNDS[r] * P
-            xr = spool.tile([P, RMAX * P], F32)
-            nc.scalar.activation(out=xr[:, 0:w], in_=pt_t[r][:, 0:w], func=ACT.Identity, bias=b_col[:, 0:1], scale=1.0)
-            xr_t[r] = xr
-
-        def tback(r):
-            pb = ps_b.tile([P, RMAX, P], F32)
-            for a in range(ROUNDS[r]):
-                nc.tensor.transpose(pb[:, a, :], xr_t[r][:, a * P : (a + 1) * P], ident[:])
-            pb_t[r] = pb
 
         def bias_add(r):
             g = group_of[r]
-            nt = ROUNDS[r]
             gn = gsize(g)
-            n0 = first[r] - first[GROUPS[g][0]]
             if r == GROUPS[g][0]:
                 o = opool.tile([P, GMAX * OUT], F32)
                 o_t[g] = o
             o = o_t[g]
-            nc.vector.tensor_tensor(
-                out=o[:, 0 : gn * P].rearrange("p (n h d) -> p n h d", h=2, d=64)[:, n0 : n0 + nt, :, 32:64],
-                in0=pn_t[r][:, 0:nt, 0:64].rearrange("p n (h c) -> p n h c", h=2),
-                in1=bb_nr[:, 0:64].rearrange("p (h c) -> p h c", h=2).unsqueeze(1).to_broadcast([P, nt, 2, 32]),
-                op=ALU.add,
-            )
-            nc.vector.tensor_tensor(
-                out=o[:, gn * 192 : gn * OUT].rearrange("p (n c) -> p n c", c=64)[:, n0 : n0 + nt, :],
-                in0=pn_t[r][:, 0:nt, 64:P],
-                in1=bb_nr[:, 64:P].unsqueeze(1).to_broadcast([P, nt, 64]),
-                op=ALU.add,
-            )
+            oq = o[:, 0 : gn * P].rearrange("p (n c) -> p n c", c=P)
+            okv = o[:, gn * P : gn * OUT].rearrange("p (s n c) -> p n s c", s=2, c=64)
+            for b, pn in enumerate(pn_t[r]):
+                nb = min(2, ROUNDS[r] - 2 * b)
+                n0 = first[r] - first[GROUPS[g][0]] + 2 * b
+                nc.vector.tensor_tensor(
+                    out=oq[:, n0 : n0 + nb],
+                    in0=pn[:, 0:nb, 0:P],
+                    in1=bb[:, 0:P].unsqueeze(1).to_broadcast([P, nb, P]),
+                    op=ALU.add,
+                )
+                nc.vector.tensor_tensor(
+                    out=okv[:, n0 : n0 + nb],
+                    in0=pn[:, 0:nb, P:OUT].rearrange("p n (s c) -> p n s c", s=2),
+                    in1=bb[:, P:OUT].rearrange("p (s c) -> p s c", s=2).unsqueeze(1).to_broadcast([P, nb, 2, 64]),
+                    op=ALU.add,
+                )
 
-        def rope_mul(r):
-            g = group_of[r]
-            nt = ROUNDS[r]
+        def parts(g):
+            return [(0, 2), (2 * gsize(g), 1)]
+
+        def rope_t1(g, part):
             gn = gsize(g)
-            i0 = first[r]
-            n0 = first[r] - first[GROUPS[g][0]]
-            if r == GROUPS[g][0]:
-                t1 = spool.tile([P, 3 * GMAX * 32], F32)
-                t2 = spool.tile([P, 3 * GMAX * 32], F32)
-                t1_t[g] = t1
-                t2_t[g] = t2
-            t1v = t1_t[g][:].rearrange("p (h n c) -> p n h c", h=3, c=32)[:, n0 : n0 + nt]
-            t2v = t2_t[g][:].rearrange("p (h n c) -> p n h c", h=3, c=32)[:, n0 : n0 + nt]
-            cosv = cos_sb[:].rearrange("p (i c) -> p i c", c=32)[:, i0 : i0 + nt, :]
-            sinv = sin_sb[:].rearrange("p (i c) -> p i c", c=32)[:, i0 : i0 + nt, :]
-            xv = pb_t[r][:, 0:nt, 0:96].rearrange("p n (h c) -> p n h c", h=3)
-            nc.vector.tensor_tensor(out=t1v, in0=xv, in1=cosv.unsqueeze(2).to_broadcast([P, nt, 3, 32]), op=ALU.mult)
+            i0 = first[GROUPS[g][0]]
+            b0, nh = part
+            xv = o_t[g][:, b0 * 64 : (b0 + nh * gn) * 64].rearrange("p (n h d) -> p n h d", h=nh, d=64)[:, :, :, 0:32]
+            tv = t1_t[g][:, b0 * 32 : (b0 + nh * gn) * 32].rearrange("p (n h c) -> p n h c", h=nh, c=32)
+            cv = cos_sb[:, i0 * 32 : (i0 + gn) * 32].rearrange("p (n c) -> p n c", c=32)
+            nc.vector.tensor_tensor(out=tv, in0=xv, in1=cv.unsqueeze(2).to_broadcast([P, gn, nh, 32]), op=ALU.mult)
+
+        def rope_t2(g, part):
+            gn = gsize(g)
+            i0 = first[GROUPS[g][0]]
+            b0, nh = part
+            xv = o_t[g][:, b0 * 64 : (b0 + nh * gn) * 64].rearrange("p (n h d) -> p n h d", h=nh, d=64)[:, :, :, 0:32]
+            tv = t2_t[g][:, b0 * 32 : (b0 + nh * gn) * 32].rearrange("p (n h c) -> p n h c", h=nh, c=32)
+            sv = sin_sb[:, i0 * 32 : (i0 + gn) * 32].rearrange("p (n c) -> p n c", c=32)
             for e in range(2):
                 lo, ot = 16 * e, 16 * (1 - e)
                 nc.vector.tensor_tensor(
-                    out=t2v[:, :, :, lo : lo + 16],
+                    out=tv[:, :, :, lo : lo + 16],
                     in0=xv[:, :, :, ot : ot + 16],
-                    in1=sinv[:, :, lo : lo + 16].unsqueeze(2).to_broadcast([P, nt, 3, 16]),
+                    in1=sv[:, :, lo : lo + 16].unsqueeze(2).to_broadcast([P, gn, nh, 16]),
                     op=ALU.mult,
                 )
-            ku_out = o_t[g][:, gn * P : gn * 192].rearrange("p (n d) -> p n d", d=64)[:, n0 : n0 + nt, 32:64]
-            if KU_ON_SCALAR:
-                nc.scalar.copy(out=ku_out, in_=pb_t[r][:, 0:nt, 96:P])
-            else:
-                nc.vector.tensor_copy(out=ku_out, in_=pb_t[r][:, 0:nt, 96:P])
 
         def rope_add(g):
             gn = gsize(g)
-            o = o_t[g]
-            for h in range(3):
-                if h < 2:
-                    dst = o[:, 0 : gn * P].rearrange("p (n h d) -> p n h d", h=2, d=64)[:, :, h, 0:32]
-                else:
-                    dst = o[:, gn * P : gn * 192].rearrange("p (n d) -> p n d", d=64)[:, :, 0:32]
-                s0 = h * GMAX * 32
-                nc.vector.tensor_tensor(
-                    out=dst.rearrange("p n (j e) -> p n j e", e=2),
-                    in0=t1_t[g][:, s0 : s0 + gn * 32].rearrange("p (n e j) -> p n j e", e=2, j=16),
-                    in1=t2_t[g][:, s0 : s0 + gn * 32].rearrange("p (n e j) -> p n j e", e=2, j=16),
-                    op=ALU.add,
-                )
+            dst = o_t[g][:, 0 : gn * 192].rearrange("p (b d) -> p b d", d=64)[:, :, 0:32]
+            nc.vector.tensor_tensor(
+                out=dst.rearrange("p b (j e) -> p b j e", e=2),
+                in0=t1_t[g][:, 0 : gn * 96].rearrange("p (b e j) -> p b j e", e=2, j=16),
+                in1=t2_t[g][:, 0 : gn * 96].rearrange("p (b e j) -> p b j e", e=2, j=16),
+                op=ALU.add,
+            )
+
+        def rope_first(g):
+            t1 = spool.tile([P, 3 * GMAX * 32], F32)
+            t2 = spool.tile([P, 3 * GMAX * 32], F32)
+            t1_t[g] = t1
+            t2_t[g] = t2
+            pq, pk = parts(g)
+            rope_t1(g, pq)
+            rope_t1(g, pk)
+            rope_t2(g, pk)
+
+        def rope_second(g):
+            pq, pk = parts(g)
+            rope_t2(g, pq)
+            rope_add(g)
+            store(g)
 
         def store(g):
             gn = gsize(g)
@@ -224,45 +208,39 @@ def tile_selfattention_pa_t_kernel(tc, hidden_states, cos, sin, W_qkv, b_qkv, ou
         ones = const.tile([P, P], BF16)
         nc.vector.memset(ones[:], 1.0)
         warm = const.tile([P, 1], F32)
-        nc.scalar.activation(out=warm[:], in_=ones[:, 0:1], func=ACT.Identity, scale=1.0)
+        nc.scalar.copy(out=warm[:], in_=ones[:, 0:1])
 
+        load(0)
         nc.sync.dma_start(out=b_row[0:1, :], in_=b_qkv.rearrange("(o c) -> o c", o=1))
         w_raw = const.tile([P, 2 * 4 * OUT], BF16)
         nc.sync.dma_start(
             out=w_raw[:].rearrange("p (g f) -> p g f", g=2),
             in_=W_qkv.rearrange("(g p t) c -> p g (t c)", g=2, t=4),
         )
+        load(1)
+        load(2)
+        load(3)
         sin_sb = const.tile([P, NT * 32], BF16)
         cos_sb = const.tile([P, NT * 32], BF16)
-        for item in HEAD:
-            if item[0] == "x":
-                load(int(item[1:]))
-            else:
-                nc.sync.dma_start(out=sin_sb[:], in_=sin.rearrange("(p i) c -> p (i c)", i=NT))
-                nc.sync.dma_start(out=cos_sb[:], in_=cos.rearrange("(p i) c -> p (i c)", i=NT))
+        nc.sync.dma_start(out=sin_sb[:], in_=sin.rearrange("(p i) c -> p (i c)", i=NT))
+        nc.sync.dma_start(out=cos_sb[:], in_=cos.rearrange("(p i) c -> p (i c)", i=NT))
+        for r in range(4, XB):
+            load(r)
 
         sneg = sin_sb[:].rearrange("p (i e j) -> p i e j", e=2, j=16)[:, :, 0, :]
         nc.gpsimd.tensor_scalar(out=sneg, in0=sneg, scalar1=-1.0, scalar2=0.0, op0=ALU.mult, op1=ALU.add)
 
-        pbias = ps_n.tile([P, RMAX, P], F32, tag="pn")
-        pb2 = pbias[:].rearrange("p a c -> p (a c)")[:, 0:OUT]
-        nc.tensor.matmul(out=pb2, lhsT=ones[:], rhs=b_row[:], start=True, stop=True)
-        pbv = pb2.rearrange("p (n m) -> p n m", n=4)
-        bb_rp = const.tile([P, P], F32)
-        bb_nr = const.tile([P, P], F32)
-        for e in range(2):
-            nc.scalar.copy(
-                out=bb_rp[:, 0:96].rearrange("p (h c) -> p h c", h=3)[:, :, 16 * e : 16 * e + 16], in_=pbv[:, 0:3, e:32:2]
-            )
-        nc.scalar.copy(out=bb_rp[:, 96:P], in_=pbv[:, 2, 32:64])
-        nc.scalar.copy(out=bb_nr[:, 0:64].rearrange("p (h c) -> p h c", h=2), in_=pbv[:, 0:2, 32:64])
-        nc.scalar.copy(out=bb_nr[:, 64:P], in_=pbv[:, 3, :])
-        b_col = const.tile([P, 1], F32)
+        bb = const.tile([P, OUT], F32)
 
-        def bias_column():
-            pbt = ps_b.tile([P, RMAX, P], F32, tag="pb")
-            nc.tensor.transpose(pbt[:, 0, :], bb_rp[:], ident[:])
-            nc.scalar.copy(out=b_col[:], in_=pbt[:, 0, 0:1])
+        def bias_prep():
+            pbias = ps_n.tile([P, 2, OUT], F32, tag="pn")
+            nc.tensor.matmul(out=pbias[:, 0, :], lhsT=ones[:], rhs=b_row[:], start=True, stop=True)
+            src = pbias[:, 0, :].rearrange("p (n m) -> p n m", n=4)
+            dst = bb[:].rearrange("p (n m) -> p n m", n=4)
+            for e in range(2):
+                nc.scalar.copy(out=dst[:, 0:3, 16 * e : 16 * e + 16], in_=src[:, 0:3, e:32:2])
+            nc.scalar.copy(out=dst[:, 0:3, 32:64], in_=src[:, 0:3, 32:64])
+            nc.scalar.copy(out=dst[:, 3, :], in_=src[:, 3, :])
 
         w_codes, w_scl = [], []
 
@@ -270,34 +248,26 @@ def tile_selfattention_pa_t_kernel(tc, hidden_states, cos, sin, W_qkv, b_qkv, ou
             for g in range(2):
                 w_grp = const.tile([P, OUT * 4], BF16, name="w_grp%d" % g, align_bytes=64)
                 src = w_raw[:, g * 1024 : (g + 1) * 1024].rearrange("p (t n m) -> p n m t", t=4, n=4)
+                dst = w_grp[:].rearrange("p (n m t) -> p n m t", n=4, t=4)
                 for e in range(2):
-                    nc.vector.tensor_copy(
-                        out=w_grp[:, 0 : 96 * 4].rearrange("p (h m t) -> p h m t", h=3, t=4)[:, :, 16 * e : 16 * e + 16, :],
-                        in_=src[:, 0:3, e:32:2, :],
-                    )
-                nc.vector.tensor_copy(
-                    out=w_grp[:, 96 * 4 : P * 4].rearrange("p (m t) -> p m t", t=4), in_=src[:, 2, 32:64, :]
-                )
-                nc.vector.tensor_copy(
-                    out=w_grp[:, P * 4 : 192 * 4].rearrange("p (h m t) -> p h m t", h=2, t=4), in_=src[:, 0:2, 32:64, :]
-                )
-                nc.vector.tensor_copy(
-                    out=w_grp[:, 192 * 4 : OUT * 4].rearrange("p (m t) -> p m t", t=4), in_=src[:, 3, :, :]
-                )
+                    nc.vector.tensor_copy(out=dst[:, 0:3, 16 * e : 16 * e + 16, :], in_=src[:, 0:3, e:32:2, :])
+                nc.vector.tensor_copy(out=dst[:, 0:3, 32:64, :], in_=src[:, 0:3, 32:64, :])
+                nc.vector.tensor_copy(out=dst[:, 3, :, :], in_=src[:, 3, :, :])
                 wc = const.tile([P, OUT], U32, name="w_codes%d" % g, align_bytes=64)
                 ws = const.tile([P, OUT], U8, name="w_scl%d" % g, align_bytes=64)
                 nc.vector.quantize_mx(out=wc[:].bitcast(FP8X4), scales=ws[:], in_=w_grp[:])
                 w_codes.append(wc)
                 w_scl.append(ws)
 
+        pending = []
         for p in range(-2, nr + 1):
             if 0 <= p + 2 < nr:
                 transp(p + 2)
                 if p + 2 + XB < nr:
                     load(p + 2 + XB)
                 copyout(p + 2)
-            if p == -1:
-                bias_column()
+            if p == -2:
+                bias_prep()
                 w_prep()
             if 0 <= p + 1 < nr:
                 quant(p + 1)
@@ -305,12 +275,13 @@ def tile_selfattention_pa_t_kernel(tc, hidden_states, cos, sin, W_qkv, b_qkv, ou
                 bias_add(p)
             if 0 <= p + 1 < nr:
                 mx(p + 1)
-                evac(p + 1)
-            if 0 <= p - 1 < nr:
-                rope_mul(p - 1)
-                g = group_of[p - 1]
-                if p - 1 == GROUPS[g][-1]:
-                    rope_add(g)
-                    store(g)
+            while pending:
+                rope_second(pending.pop())
             if 0 <= p < nr:
-                tback(p)
+                g = group_of[p]
+                if p == GROUPS[g][-1]:
+                    rope_first(g)
+                    if p >= 17:
+                        rope_second(g)
+                    else:
+                        pending.append(g)

@@ -16,17 +16,24 @@ T, H, OUT = 8192, 1024, 256
 NT = T // P
 FLOPS = 2 * T * H * OUT
 
-ROUNDS = [1, 1, 2] + [4] * 14 + [2, 1, 1]
-GROUPS = [[0, 1, 2]] + [[3 + 2 * g, 4 + 2 * g] for g in range(7)] + [[17], [18], [19]]
+LOADS = [1, 1, 2] + [4] * 14 + [2, 1, 1]
+STEPS = [1, 1] + [2] * 30 + [1, 1]
+GROUPS = [[0, 1, 2]] + [[3 + 4 * g + j for j in range(4)] for g in range(7)] + [[31], [32], [33]]
 XB = 8
-RMAX = 4
+LMAX = 4
+SMAX = 2
 GMAX = 8
 
 
 def tile_selfattention_pa_t_kernel(tc, hidden_states, cos, sin, W_qkv, b_qkv, out_0, out_1, out_2):
     nc = tc.nc
-    nr = len(ROUNDS)
-    first = [sum(ROUNDS[:r]) for r in range(nr)]
+    ns = len(STEPS)
+    first = [sum(STEPS[:s]) for s in range(ns)]
+    lfirst = [sum(LOADS[:c]) for c in range(len(LOADS))]
+    chunk_of = {}
+    for c, n in enumerate(LOADS):
+        for a in range(n):
+            chunk_of[lfirst[c] + a] = (c, a)
     group_of = {}
     for g, rs in enumerate(GROUPS):
         for r in rs:
@@ -49,91 +56,87 @@ def tile_selfattention_pa_t_kernel(tc, hidden_states, cos, sin, W_qkv, b_qkv, ou
         x_t, xt_t, grp_t, codes_t, scl_t, pn_t, o_t, t1_t, t2_t = {}, {}, {}, {}, {}, {}, {}, {}, {}
 
         def gsize(g):
-            return sum([ROUNDS[j] for j in GROUPS[g]])
+            return sum([STEPS[j] for j in GROUPS[g]])
 
-        def load(r):
-            nt = ROUNDS[r]
-            xc = xpool.tile([P, RMAX * H], BF16)
+        def load(c):
+            n = LOADS[c]
+            xc = xpool.tile([P, LMAX * H], BF16)
             nc.sync.dma_start(
-                out=xc[:, 0 : nt * H].rearrange("p (n k) -> p n k", k=H),
-                in_=x_v[:, first[r] : first[r] + nt, :],
+                out=xc[:, 0 : n * H].rearrange("p (n k) -> p n k", k=H),
+                in_=x_v[:, lfirst[c] : lfirst[c] + n, :],
             )
-            x_t[r] = xc
+            x_t[c] = xc
 
-        def transp(r):
-            xw = x_t[r][:].bitcast(F32)
-            xt_t[r] = []
-            for a in range(ROUNDS[r]):
+        def transp(s):
+            xt_t[s] = []
+            for a in range(STEPS[s]):
+                c, ca = chunk_of[first[s] + a]
+                xw = x_t[c][:].bitcast(F32)
                 xt = ps_x.tile([P, 4, P], F32)
                 for b in range(4):
-                    w0 = a * 512 + (b // 2) * 256 + b % 2
+                    w0 = ca * 512 + (b // 2) * 256 + b % 2
                     nc.tensor.transpose(xt[:, b, :], xw[:, w0 : w0 + 255 : 2], ident[:])
-                xt_t[r].append(xt)
+                xt_t[s].append(xt)
 
-        def copyout(r):
-            nt = ROUNDS[r]
-            grp = gpool.tile([P, RMAX * H], BF16, align_bytes=64)
+        def copyout(s):
+            nt = STEPS[s]
+            grp = gpool.tile([P, SMAX * H], BF16, align_bytes=64)
             gw = grp[:].bitcast(F32)[:, 0 : nt * 512].rearrange("p (g a m u) -> p g a m u", g=2, a=nt, u=2)
             for a in range(nt):
-                nc.scalar.copy(out=gw[:, :, a], in_=xt_t[r][a][:].rearrange("p (g u) m -> p g m u", u=2))
-            grp_t[r] = grp
+                nc.scalar.copy(out=gw[:, :, a], in_=xt_t[s][a][:].rearrange("p (g u) m -> p g m u", u=2))
+            grp_t[s] = grp
 
-        def quant(r):
-            nt = ROUNDS[r]
-            codes = gpool.tile([P, RMAX * 256], U32, align_bytes=64)
-            scl = gpool.tile([P, RMAX * 256], U8, align_bytes=64)
+        def quant(s):
+            nt = STEPS[s]
+            codes = gpool.tile([P, SMAX * 256], U32, align_bytes=64)
+            scl = gpool.tile([P, SMAX * 256], U8, align_bytes=64)
             nc.vector.quantize_mx(
                 out=codes[:, 0 : nt * 256].bitcast(FP8X4),
                 scales=scl[:, 0 : nt * 256],
-                in_=grp_t[r][:, 0 : nt * H],
+                in_=grp_t[s][:, 0 : nt * H],
             )
-            codes_t[r] = codes
-            scl_t[r] = scl
+            codes_t[s] = codes
+            scl_t[s] = scl
 
-        def mx(r):
-            nt = ROUNDS[r]
-            w = nt * P
-            pn_t[r] = []
-            for a in range(nt):
-                if a % 2 == 0:
-                    pn = ps_n.tile([P, 2, OUT], F32)
-                    pn_t[r].append(pn)
+        def mx(s):
+            w = STEPS[s] * P
+            pn = ps_n.tile([P, 2, OUT], F32)
+            for a in range(STEPS[s]):
                 for g in range(2):
                     s0 = g * w + a * P
                     nc.tensor.matmul_mx(
-                        out=pn[:, a % 2, :],
-                        lhsT=codes_t[r][:, s0 : s0 + P].bitcast(FP8X4),
-                        lhsT_scale=scl_t[r][:, s0 : s0 + P],
+                        out=pn[:, a, :],
+                        lhsT=codes_t[s][:, s0 : s0 + P].bitcast(FP8X4),
+                        lhsT_scale=scl_t[s][:, s0 : s0 + P],
                         rhs=w_codes[g][:].bitcast(FP8X4),
                         rhs_scale=w_scl[g][:],
                         start=(g == 0),
                         stop=(g == 1),
                     )
+            pn_t[s] = pn
 
-        def bias_add(r):
-            g = group_of[r]
+        def bias_add(s):
+            g = group_of[s]
             gn = gsize(g)
-            if r == GROUPS[g][0]:
+            nb = STEPS[s]
+            n0 = first[s] - first[GROUPS[g][0]]
+            if s == GROUPS[g][0]:
                 o = opool.tile([P, GMAX * OUT], F32)
                 o_t[g] = o
             o = o_t[g]
-            oq = o[:, 0 : gn * P].rearrange("p (n c) -> p n c", c=P)
-            okv = o[:, gn * P : gn * OUT].rearrange("p (s n c) -> p n s c", s=2, c=64)
-            for b, pn in enumerate(pn_t[r]):
-                nb = min(2, ROUNDS[r] - 2 * b)
-                n0 = first[r] - first[GROUPS[g][0]] + 2 * b
-                nc.vector.tensor_tensor(
-                    out=oq[:, n0 : n0 + nb],
-                    in0=pn[:, 0:nb, 0:P],
-                    in1=bb[:, 0:P].unsqueeze(1).to_broadcast([P, nb, P]),
-                    op=ALU.add,
-                )
-                nc.vector.tensor_tensor(
-                    out=okv[:, n0 : n0 + nb],
-                    in0=pn[:, 0:nb, P:OUT].rearrange("p n (s c) -> p n s c", s=2),
-                    in1=bb[:, P:OUT].rearrange("p (s c) -> p s c", s=2).unsqueeze(1).to_broadcast([P, nb, 2, 64]),
-                    op=ALU.add,
-                )
+            pn = pn_t[s]
+            nc.vector.tensor_tensor(
+                out=o[:, 0 : gn * P].rearrange("p (n c) -> p n c", c=P)[:, n0 : n0 + nb],
+                in0=pn[:, 0:nb, 0:P],
+                in1=bb[:, 0:P].unsqueeze(1).to_broadcast([P, nb, P]),
+                op=ALU.add,
+            )
+            nc.vector.tensor_tensor(
+                out=o[:, gn * P : gn * OUT].rearrange("p (s n c) -> p n s c", s=2, c=64)[:, n0 : n0 + nb],
+                in0=pn[:, 0:nb, P:OUT].rearrange("p n (s c) -> p n s c", s=2),
+                in1=bb[:, P:OUT].rearrange("p (s c) -> p s c", s=2).unsqueeze(1).to_broadcast([P, nb, 2, 64]),
+                op=ALU.add,
+            )
 
         def parts(g):
             return [(0, 2), (2 * gsize(g), 1)]
@@ -173,21 +176,25 @@ def tile_selfattention_pa_t_kernel(tc, hidden_states, cos, sin, W_qkv, b_qkv, ou
                 op=ALU.add,
             )
 
-        def rope_first(g):
+        def rope_start(g):
             t1 = spool.tile([P, 3 * GMAX * 32], F32)
             t2 = spool.tile([P, 3 * GMAX * 32], F32)
             t1_t[g] = t1
             t2_t[g] = t2
-            pq, pk = parts(g)
-            rope_t1(g, pq)
-            rope_t1(g, pk)
-            rope_t2(g, pk)
 
-        def rope_second(g):
+        def rope_piece(g, j):
             pq, pk = parts(g)
-            rope_t2(g, pq)
-            rope_add(g)
-            store(g)
+            if j == 0:
+                rope_start(g)
+                rope_t1(g, pq)
+            elif j == 1:
+                rope_t2(g, pq)
+            elif j == 2:
+                rope_t1(g, pk)
+                rope_t2(g, pk)
+            else:
+                rope_add(g)
+                store(g)
 
         def store(g):
             gn = gsize(g)
@@ -259,29 +266,29 @@ def tile_selfattention_pa_t_kernel(tc, hidden_states, cos, sin, W_qkv, b_qkv, ou
                 w_codes.append(wc)
                 w_scl.append(ws)
 
+        loaded = XB
         pending = []
-        for p in range(-2, nr + 1):
-            if 0 <= p + 2 < nr:
-                transp(p + 2)
-                if p + 2 + XB < nr:
-                    load(p + 2 + XB)
-                copyout(p + 2)
-            if p == -2:
+        for s in range(-2, ns + 1):
+            if 0 <= s + 2 < ns:
+                transp(s + 2)
+                copyout(s + 2)
+                c, ca = chunk_of[first[s + 2] + STEPS[s + 2] - 1]
+                if ca == LOADS[c] - 1 and loaded < len(LOADS):
+                    load(loaded)
+                    loaded += 1
+            if s == -2:
                 bias_prep()
                 w_prep()
-            if 0 <= p + 1 < nr:
-                quant(p + 1)
-            if 0 <= p < nr:
-                bias_add(p)
-            if 0 <= p + 1 < nr:
-                mx(p + 1)
-            while pending:
-                rope_second(pending.pop())
-            if 0 <= p < nr:
-                g = group_of[p]
-                if p == GROUPS[g][-1]:
-                    rope_first(g)
-                    if p >= 17:
-                        rope_second(g)
-                    else:
-                        pending.append(g)
+            if 0 <= s + 1 < ns:
+                quant(s + 1)
+            if 0 <= s < ns:
+                mx(s)
+            if 0 <= s - 1 < ns:
+                bias_add(s - 1)
+            for j in range(len(pending) if s > ns - 4 else min(1, len(pending))):
+                rope_piece(*pending.pop(0))
+            if 0 <= s - 1 < ns and s - 1 == GROUPS[group_of[s - 1]][-1]:
+                for j in range(4):
+                    pending.append((group_of[s - 1], j))
+        while pending:
+            rope_piece(*pending.pop(0))

@@ -147,7 +147,7 @@ def tile_selfattention_pa_t_kernel(tc, hidden_states, cos, sin, W_qkv, b_qkv, ou
             b0, nh = part
             xv = o_t[g][:, b0 * 64 : (b0 + nh * gn) * 64].rearrange("p (n h d) -> p n h d", h=nh, d=64)[:, :, :, 0:32]
             tv = t1_t[g][:, b0 * 32 : (b0 + nh * gn) * 32].rearrange("p (n h c) -> p n h c", h=nh, c=32)
-            cv = cos_sb[:, i0 * 32 : (i0 + gn) * 32].rearrange("p (n c) -> p n c", c=32)
+            cv = cos_i[:, i0 * 32 : (i0 + gn) * 32].rearrange("p (n c) -> p n c", c=32)
             nc.vector.tensor_tensor(out=tv, in0=xv, in1=cv.unsqueeze(2).to_broadcast([P, gn, nh, 32]), op=ALU.mult)
 
         def rope_t2(g, part):
@@ -155,24 +155,19 @@ def tile_selfattention_pa_t_kernel(tc, hidden_states, cos, sin, W_qkv, b_qkv, ou
             i0 = first[GROUPS[g][0]]
             b0, nh = part
             xv = o_t[g][:, b0 * 64 : (b0 + nh * gn) * 64].rearrange("p (n h d) -> p n h d", h=nh, d=64)[:, :, :, 0:32]
-            tv = t2_t[g][:, b0 * 32 : (b0 + nh * gn) * 32].rearrange("p (n h c) -> p n h c", h=nh, c=32)
-            sv = sin_sb[:, i0 * 32 : (i0 + gn) * 32].rearrange("p (n c) -> p n c", c=32)
-            for e in range(2):
-                lo, ot = 16 * e, 16 * (1 - e)
-                nc.vector.tensor_tensor(
-                    out=tv[:, :, :, lo : lo + 16],
-                    in0=xv[:, :, :, ot : ot + 16],
-                    in1=sv[:, :, lo : lo + 16].unsqueeze(2).to_broadcast([P, gn, nh, 16]),
-                    op=ALU.mult,
-                )
+            tv = t2_t[g][:, b0 * 32 : (b0 + nh * gn) * 32].rearrange("p (n h j e) -> p n h j e", h=nh, j=16, e=2)
+            sv = sin_i[:, i0 * 32 : (i0 + gn) * 32].rearrange("p (n j e) -> p n j e", j=16, e=2)
+            xs = xv.rearrange("p n h (j e) -> p n h j e", e=2)[:, :, :, :, ::-1]
+            for h in range(nh):
+                nc.vector.tensor_tensor(out=tv[:, :, h], in0=xs[:, :, h], in1=sv, op=ALU.mult)
 
         def rope_add(g):
             gn = gsize(g)
             dst = o_t[g][:, 0 : gn * 192].rearrange("p (b d) -> p b d", d=64)[:, :, 0:32]
             nc.vector.tensor_tensor(
-                out=dst.rearrange("p b (j e) -> p b j e", e=2),
-                in0=t1_t[g][:, 0 : gn * 96].rearrange("p (b e j) -> p b j e", e=2, j=16),
-                in1=t2_t[g][:, 0 : gn * 96].rearrange("p (b e j) -> p b j e", e=2, j=16),
+                out=dst,
+                in0=t1_t[g][:, 0 : gn * 96].rearrange("p (b c) -> p b c", c=32),
+                in1=t2_t[g][:, 0 : gn * 96].rearrange("p (b c) -> p b c", c=32),
                 op=ALU.add,
             )
 
@@ -237,29 +232,33 @@ def tile_selfattention_pa_t_kernel(tc, hidden_states, cos, sin, W_qkv, b_qkv, ou
         sneg = sin_sb[:].rearrange("p (i e j) -> p i e j", e=2, j=16)[:, :, 0, :]
         nc.gpsimd.tensor_scalar(out=sneg, in0=sneg, scalar1=-1.0, scalar2=0.0, op0=ALU.mult, op1=ALU.add)
 
+        cos_i = const.tile([P, NT * 32], BF16)
+        sin_i = const.tile([P, NT * 32], BF16)
+
+        def tables(g):
+            lo, hi = first[GROUPS[g][0]] * 32, (first[GROUPS[g][0]] + gsize(g)) * 32
+            for dst, src in ((cos_i, cos_sb), (sin_i, sin_sb)):
+                nc.scalar.copy(
+                    out=dst[:, lo:hi].rearrange("p (i j e) -> p i j e", j=16, e=2),
+                    in_=src[:, lo:hi].rearrange("p (i e j) -> p i j e", e=2, j=16),
+                )
+
         bb = const.tile([P, OUT], F32)
 
         def bias_prep():
             pbias = ps_n.tile([P, 2, OUT], F32, tag="pn")
             nc.tensor.matmul(out=pbias[:, 0, :], lhsT=ones[:], rhs=b_row[:], start=True, stop=True)
-            src = pbias[:, 0, :].rearrange("p (n m) -> p n m", n=4)
-            dst = bb[:].rearrange("p (n m) -> p n m", n=4)
-            for e in range(2):
-                nc.scalar.copy(out=dst[:, 0:3, 16 * e : 16 * e + 16], in_=src[:, 0:3, e:32:2])
-            nc.scalar.copy(out=dst[:, 0:3, 32:64], in_=src[:, 0:3, 32:64])
-            nc.scalar.copy(out=dst[:, 3, :], in_=src[:, 3, :])
+            nc.scalar.copy(out=bb[:], in_=pbias[:, 0, :])
 
         w_codes, w_scl = [], []
 
         def w_prep():
             for g in range(2):
                 w_grp = const.tile([P, OUT * 4], BF16, name="w_grp%d" % g, align_bytes=64)
-                src = w_raw[:, g * 1024 : (g + 1) * 1024].rearrange("p (t n m) -> p n m t", t=4, n=4)
-                dst = w_grp[:].rearrange("p (n m t) -> p n m t", n=4, t=4)
-                for e in range(2):
-                    nc.vector.tensor_copy(out=dst[:, 0:3, 16 * e : 16 * e + 16, :], in_=src[:, 0:3, e:32:2, :])
-                nc.vector.tensor_copy(out=dst[:, 0:3, 32:64, :], in_=src[:, 0:3, 32:64, :])
-                nc.vector.tensor_copy(out=dst[:, 3, :, :], in_=src[:, 3, :, :])
+                nc.vector.tensor_copy(
+                    out=w_grp[:].rearrange("p (c t) -> p c t", t=4),
+                    in_=w_raw[:, g * 1024 : (g + 1) * 1024].rearrange("p (t c) -> p c t", t=4),
+                )
                 wc = const.tile([P, OUT], U32, name="w_codes%d" % g, align_bytes=64)
                 ws = const.tile([P, OUT], U8, name="w_scl%d" % g, align_bytes=64)
                 nc.vector.quantize_mx(out=wc[:].bitcast(FP8X4), scales=ws[:], in_=w_grp[:])
@@ -279,6 +278,8 @@ def tile_selfattention_pa_t_kernel(tc, hidden_states, cos, sin, W_qkv, b_qkv, ou
             if s == -2:
                 bias_prep()
                 w_prep()
+            if 0 <= s < ns and s == GROUPS[group_of[s]][-1]:
+                tables(group_of[s])
             if 0 <= s + 1 < ns:
                 quant(s + 1)
             if 0 <= s < ns:

@@ -16,10 +16,10 @@ T, H, OUT = 8192, 1024, 256
 NT = T // P
 FLOPS = 2 * T * H * OUT
 
-LOADS = [1, 1, 2] + [4] * 14 + [2, 1, 1]
+LOADS = [1, 1, 2, 2, 2] + [4] * 13 + [2, 1, 1]
 STEPS = [1, 1] + [2] * 30 + [1, 1]
 GROUPS = [[0, 1, 2]] + [[3 + 4 * g + j for j in range(4)] for g in range(7)] + [[31], [32], [33]]
-XB = 8
+XB = 6
 LMAX = 4
 SMAX = 2
 GMAX = 8
@@ -48,7 +48,7 @@ def tile_selfattention_pa_t_kernel(tc, hidden_states, cos, sin, W_qkv, b_qkv, ou
         const = ctx.enter_context(tc.tile_pool(name="const", bufs=1))
         xpool = ctx.enter_context(tc.tile_pool(name="xpool", bufs=XB))
         gpool = ctx.enter_context(tc.tile_pool(name="gpool", bufs=4))
-        opool = ctx.enter_context(tc.tile_pool(name="opool", bufs=4))
+        opool = ctx.enter_context(tc.tile_pool(name="opool", bufs=6))
         spool = ctx.enter_context(tc.tile_pool(name="spool", bufs=2))
         ps_x = ctx.enter_context(tc.psum_pool(name="ps_x", bufs=4))
         ps_n = ctx.enter_context(tc.psum_pool(name="ps_n", bufs=4))
@@ -219,18 +219,22 @@ def tile_selfattention_pa_t_kernel(tc, hidden_states, cos, sin, W_qkv, b_qkv, ou
             out=w_raw[:].rearrange("p (g f) -> p g f", g=2),
             in_=W_qkv.rearrange("(g p t) c -> p g (t c)", g=2, t=4),
         )
-        load(1)
-        load(2)
-        load(3)
         sin_sb = const.tile([P, NT * 32], BF16)
         cos_sb = const.tile([P, NT * 32], BF16)
-        nc.sync.dma_start(out=sin_sb[:], in_=sin.rearrange("(p i) c -> p (i c)", i=NT))
-        nc.sync.dma_start(out=cos_sb[:], in_=cos.rearrange("(p i) c -> p (i c)", i=NT))
-        for r in range(4, XB):
-            load(r)
 
-        sneg = sin_sb[:].rearrange("p (i e j) -> p i e j", e=2, j=16)[:, :, 0, :]
-        nc.gpsimd.tensor_scalar(out=sneg, in0=sneg, scalar1=-1.0, scalar2=0.0, op0=ALU.mult, op1=ALU.add)
+        def load_tables(lo, hi):
+            for dst, src in ((sin_sb, sin), (cos_sb, cos)):
+                nc.sync.dma_start(
+                    out=dst[:, lo * 32 : hi * 32].rearrange("p (i c) -> p i c", c=32),
+                    in_=src.rearrange("(p i) c -> p i c", i=NT)[:, lo:hi, :],
+                )
+            sneg = sin_sb[:, lo * 32 : hi * 32].rearrange("p (i e j) -> p i e j", e=2, j=16)[:, :, 0, :]
+            nc.gpsimd.tensor_scalar(out=sneg, in0=sneg, scalar1=-1.0, scalar2=0.0, op0=ALU.mult, op1=ALU.add)
+
+        for c in range(1, 5):
+            load(c)
+        load_tables(0, 20)
+        load(5)
 
         cos_i = const.tile([P, NT * 32], BF16)
         sin_i = const.tile([P, NT * 32], BF16)
@@ -275,6 +279,8 @@ def tile_selfattention_pa_t_kernel(tc, hidden_states, cos, sin, W_qkv, b_qkv, ou
                 if ca == LOADS[c] - 1 and loaded < len(LOADS):
                     load(loaded)
                     loaded += 1
+                    if loaded == 8:
+                        load_tables(20, NT)
             if s == -2:
                 bias_prep()
                 w_prep()

@@ -49,7 +49,7 @@ def tile_selfattention_pa_t_kernel(tc, hidden_states, cos, sin, W_qkv, b_qkv, ou
         xpool = ctx.enter_context(tc.tile_pool(name="xpool", bufs=XB))
         gpool = ctx.enter_context(tc.tile_pool(name="gpool", bufs=4))
         opool = ctx.enter_context(tc.tile_pool(name="opool", bufs=6))
-        spool = ctx.enter_context(tc.tile_pool(name="spool", bufs=2))
+        spool = ctx.enter_context(tc.tile_pool(name="spool", bufs=4))
         ps_x = ctx.enter_context(tc.psum_pool(name="ps_x", bufs=4))
         ps_n = ctx.enter_context(tc.psum_pool(name="ps_n", bufs=4))
 
@@ -138,58 +138,45 @@ def tile_selfattention_pa_t_kernel(tc, hidden_states, cos, sin, W_qkv, b_qkv, ou
                 op=ALU.add,
             )
 
-        def parts(g):
-            return [(0, 2), (2 * gsize(g), 1)]
-
-        def rope_t1(g, part):
+        def halves(s):
+            g = group_of[s]
             gn = gsize(g)
-            i0 = first[GROUPS[g][0]]
-            b0, nh = part
-            xv = o_t[g][:, b0 * 64 : (b0 + nh * gn) * 64].rearrange("p (n h d) -> p n h d", h=nh, d=64)[:, :, :, 0:32]
-            tv = t1_t[g][:, b0 * 32 : (b0 + nh * gn) * 32].rearrange("p (n h c) -> p n h c", h=nh, c=32)
-            cv = cos_i[:, i0 * 32 : (i0 + gn) * 32].rearrange("p (n c) -> p n c", c=32)
-            nc.vector.tensor_tensor(out=tv, in0=xv, in1=cv.unsqueeze(2).to_broadcast([P, gn, nh, 32]), op=ALU.mult)
+            nb = STEPS[s]
+            n0 = first[s] - first[GROUPS[g][0]]
+            out = []
+            for lo, t0, nh in ((2 * n0, 0, 2), (2 * gn + n0, 2 * nb, 1)):
+                blocks = o_t[g][:, lo * 64 : (lo + nh * nb) * 64]
+                out.append((blocks.rearrange("p (n h d) -> p n h d", h=nh, d=64)[:, :, :, 0:32], t0, nh))
+            return out
 
-        def rope_t2(g, part):
-            gn = gsize(g)
-            i0 = first[GROUPS[g][0]]
-            b0, nh = part
-            xv = o_t[g][:, b0 * 64 : (b0 + nh * gn) * 64].rearrange("p (n h d) -> p n h d", h=nh, d=64)[:, :, :, 0:32]
-            tv = t2_t[g][:, b0 * 32 : (b0 + nh * gn) * 32].rearrange("p (n h j e) -> p n h j e", h=nh, j=16, e=2)
-            sv = sin_i[:, i0 * 32 : (i0 + gn) * 32].rearrange("p (n j e) -> p n j e", j=16, e=2)
-            xs = xv.rearrange("p n h (j e) -> p n h j e", e=2)[:, :, :, :, ::-1]
-            for h in range(nh):
-                nc.vector.tensor_tensor(out=tv[:, :, h], in0=xs[:, :, h], in1=sv, op=ALU.mult)
+        def rope_mul(s):
+            nb = STEPS[s]
+            i0 = first[s]
+            t1 = spool.tile([P, 3 * SMAX * 32], F32)
+            t2 = spool.tile([P, 3 * SMAX * 32], F32)
+            t1_t[s] = t1
+            t2_t[s] = t2
+            cv = cos_i[:, i0 * 32 : (i0 + nb) * 32].rearrange("p (n c) -> p n c", c=32)
+            sv = sin_i[:, i0 * 32 : (i0 + nb) * 32].rearrange("p (n j e) -> p n j e", j=16, e=2)
+            for xv, t0, nh in halves(s):
+                tv = t1[:, t0 * 32 : (t0 + nh * nb) * 32].rearrange("p (n h c) -> p n h c", h=nh, c=32)
+                nc.vector.tensor_tensor(out=tv, in0=xv, in1=cv.unsqueeze(2).to_broadcast([P, nb, nh, 32]), op=ALU.mult)
+            for xv, t0, nh in halves(s):
+                tv = t2[:, t0 * 32 : (t0 + nh * nb) * 32].rearrange("p (n h j e) -> p n h j e", h=nh, j=16, e=2)
+                xs = xv.rearrange("p n h (j e) -> p n h j e", e=2)[:, :, :, :, ::-1]
+                for h in range(nh):
+                    nc.vector.tensor_tensor(out=tv[:, :, h], in0=xs[:, :, h], in1=sv, op=ALU.mult)
 
-        def rope_add(g):
-            gn = gsize(g)
-            dst = o_t[g][:, 0 : gn * 192].rearrange("p (b d) -> p b d", d=64)[:, :, 0:32]
-            nc.vector.tensor_tensor(
-                out=dst,
-                in0=t1_t[g][:, 0 : gn * 96].rearrange("p (b c) -> p b c", c=32),
-                in1=t2_t[g][:, 0 : gn * 96].rearrange("p (b c) -> p b c", c=32),
-                op=ALU.add,
-            )
-
-        def rope_start(g):
-            t1 = spool.tile([P, 3 * GMAX * 32], F32)
-            t2 = spool.tile([P, 3 * GMAX * 32], F32)
-            t1_t[g] = t1
-            t2_t[g] = t2
-
-        def rope_piece(g, j):
-            pq, pk = parts(g)
-            if j == 0:
-                rope_start(g)
-                rope_t1(g, pq)
-            elif j == 1:
-                rope_t2(g, pq)
-            elif j == 2:
-                rope_t1(g, pk)
-                rope_t2(g, pk)
-            else:
-                rope_add(g)
-                store(g)
+        def rope_add(s):
+            nb = STEPS[s]
+            for xv, t0, nh in halves(s):
+                lo, hi = t0 * 32, (t0 + nh * nb) * 32
+                nc.gpsimd.tensor_tensor(
+                    out=xv,
+                    in0=t1_t[s][:, lo:hi].rearrange("p (n h c) -> p n h c", h=nh, c=32),
+                    in1=t2_t[s][:, lo:hi].rearrange("p (n h c) -> p n h c", h=nh, c=32),
+                    op=ALU.add,
+                )
 
         def store(g):
             gn = gsize(g)
@@ -270,8 +257,7 @@ def tile_selfattention_pa_t_kernel(tc, hidden_states, cos, sin, W_qkv, b_qkv, ou
                 w_scl.append(ws)
 
         loaded = XB
-        pending = []
-        for s in range(-2, ns + 1):
+        for s in range(-2, ns + 3):
             if 0 <= s + 2 < ns:
                 transp(s + 2)
                 copyout(s + 2)
@@ -284,18 +270,16 @@ def tile_selfattention_pa_t_kernel(tc, hidden_states, cos, sin, W_qkv, b_qkv, ou
             if s == -2:
                 bias_prep()
                 w_prep()
-            if 0 <= s < ns and s == GROUPS[group_of[s]][-1]:
+            if 0 <= s < ns and s == GROUPS[group_of[s]][-1 if s < 3 else 0]:
                 tables(group_of[s])
+            if 0 <= s - 3 < ns:
+                rope_mul(s - 3)
+                rope_add(s - 3)
+                if s - 3 == GROUPS[group_of[s - 3]][-1]:
+                    store(group_of[s - 3])
             if 0 <= s + 1 < ns:
                 quant(s + 1)
             if 0 <= s < ns:
                 mx(s)
             if 0 <= s - 1 < ns:
                 bias_add(s - 1)
-            for j in range(len(pending) if s > ns - 4 else min(1, len(pending))):
-                rope_piece(*pending.pop(0))
-            if 0 <= s - 1 < ns and s - 1 == GROUPS[group_of[s - 1]][-1]:
-                for j in range(4):
-                    pending.append((group_of[s - 1], j))
-        while pending:
-            rope_piece(*pending.pop(0))

@@ -16,28 +16,15 @@ T, H, OUT = 8192, 1024, 256
 NT = T // P
 FLOPS = 2 * T * H * OUT
 
-LOADS = [1, 1, 2, 2, 2] + [4] * 13 + [2, 1, 1]
-STEPS = [1, 1] + [2] * 30 + [1, 1]
-GROUPS = [[0, 1, 2]] + [[3 + 4 * g + j for j in range(4)] for g in range(7)] + [[31], [32], [33]]
+STEPS = [1, 1, 2, 2, 2] + [4] * 13 + [2, 1, 1]
 XB = 6
-LMAX = 4
-SMAX = 2
-GMAX = 8
+SMAX = 4
 
 
 def tile_selfattention_pa_t_kernel(tc, hidden_states, cos, sin, W_qkv, b_qkv, out_0, out_1, out_2):
     nc = tc.nc
     ns = len(STEPS)
     first = [sum(STEPS[:s]) for s in range(ns)]
-    lfirst = [sum(LOADS[:c]) for c in range(len(LOADS))]
-    chunk_of = {}
-    for c, n in enumerate(LOADS):
-        for a in range(n):
-            chunk_of[lfirst[c] + a] = (c, a)
-    group_of = {}
-    for g, rs in enumerate(GROUPS):
-        for r in rs:
-            group_of[r] = g
     x_v = hidden_states.rearrange("(p i) k -> p i k", i=NT)
     q_v = out_0.rearrange("(p i) h d -> p i (h d)", i=NT)
     k_v = out_1.rearrange("(p i) h d -> p i (h d)", i=NT)
@@ -48,147 +35,128 @@ def tile_selfattention_pa_t_kernel(tc, hidden_states, cos, sin, W_qkv, b_qkv, ou
         const = ctx.enter_context(tc.tile_pool(name="const", bufs=1))
         xpool = ctx.enter_context(tc.tile_pool(name="xpool", bufs=XB))
         gpool = ctx.enter_context(tc.tile_pool(name="gpool", bufs=4))
-        opool = ctx.enter_context(tc.tile_pool(name="opool", bufs=6))
+        opool = ctx.enter_context(tc.tile_pool(name="opool", bufs=8))
         spool = ctx.enter_context(tc.tile_pool(name="spool", bufs=4))
         ps_x = ctx.enter_context(tc.psum_pool(name="ps_x", bufs=4))
         ps_n = ctx.enter_context(tc.psum_pool(name="ps_n", bufs=4))
 
         x_t, xt_t, grp_t, codes_t, scl_t, pn_t, o_t, t1_t, t2_t = {}, {}, {}, {}, {}, {}, {}, {}, {}
 
-        def gsize(g):
-            return sum([STEPS[j] for j in GROUPS[g]])
-
-        def load(c):
-            n = LOADS[c]
-            xc = xpool.tile([P, LMAX * H], BF16)
+        def load(s):
+            n = STEPS[s]
+            xc = xpool.tile([P, SMAX * H], BF16)
             nc.sync.dma_start(
                 out=xc[:, 0 : n * H].rearrange("p (n k) -> p n k", k=H),
-                in_=x_v[:, lfirst[c] : lfirst[c] + n, :],
+                in_=x_v[:, first[s] : first[s] + n, :],
             )
-            x_t[c] = xc
+            x_t[s] = xc
 
-        def transp(s):
-            xt_t[s] = []
-            for a in range(STEPS[s]):
-                c, ca = chunk_of[first[s] + a]
-                xw = x_t[c][:].bitcast(F32)
-                xt = ps_x.tile([P, 4, P], F32)
-                for b in range(4):
-                    w0 = ca * 512 + (b // 2) * 256 + b % 2
-                    nc.tensor.transpose(xt[:, b, :], xw[:, w0 : w0 + 255 : 2], ident[:])
-                xt_t[s].append(xt)
+        def transp(s, a):
+            xw = x_t[s][:].bitcast(F32)
+            xt = ps_x.tile([P, 4, P], F32)
+            for b in range(4):
+                w0 = a * 512 + (b // 2) * 256 + b % 2
+                nc.tensor.transpose(xt[:, b, :], xw[:, w0 : w0 + 255 : 2], ident[:])
+            xt_t[s, a] = xt
 
-        def copyout(s):
-            nt = STEPS[s]
-            grp = gpool.tile([P, SMAX * H], BF16, align_bytes=64)
-            gw = grp[:].bitcast(F32)[:, 0 : nt * 512].rearrange("p (g a m u) -> p g a m u", g=2, a=nt, u=2)
-            for a in range(nt):
-                nc.scalar.copy(out=gw[:, :, a], in_=xt_t[s][a][:].rearrange("p (g u) m -> p g m u", u=2))
-            grp_t[s] = grp
+        def copyout(s, a):
+            n = STEPS[s]
+            if a == 0:
+                grp = gpool.tile([P, SMAX * H], BF16, align_bytes=64)
+                grp_t[s] = grp
+            gw = grp_t[s][:].bitcast(F32)[:, 0 : n * 512].rearrange("p (g a m u) -> p g a m u", g=2, a=n, u=2)
+            nc.scalar.copy(out=gw[:, :, a], in_=xt_t[s, a][:].rearrange("p (g u) m -> p g m u", u=2))
 
         def quant(s):
-            nt = STEPS[s]
+            n = STEPS[s]
             codes = gpool.tile([P, SMAX * 256], U32, align_bytes=64)
             scl = gpool.tile([P, SMAX * 256], U8, align_bytes=64)
             nc.vector.quantize_mx(
-                out=codes[:, 0 : nt * 256].bitcast(FP8X4),
-                scales=scl[:, 0 : nt * 256],
-                in_=grp_t[s][:, 0 : nt * H],
+                out=codes[:, 0 : n * 256].bitcast(FP8X4),
+                scales=scl[:, 0 : n * 256],
+                in_=grp_t[s][:, 0 : n * H],
             )
             codes_t[s] = codes
             scl_t[s] = scl
 
-        def mx(s):
-            w = STEPS[s] * P
-            pn = ps_n.tile([P, 2, OUT], F32)
-            for a in range(STEPS[s]):
-                for g in range(2):
-                    s0 = g * w + a * P
-                    nc.tensor.matmul_mx(
-                        out=pn[:, a, :],
-                        lhsT=codes_t[s][:, s0 : s0 + P].bitcast(FP8X4),
-                        lhsT_scale=scl_t[s][:, s0 : s0 + P],
-                        rhs=w_codes[g][:].bitcast(FP8X4),
-                        rhs_scale=w_scl[g][:],
-                        start=(g == 0),
-                        stop=(g == 1),
-                    )
-            pn_t[s] = pn
+        def mx(s, a):
+            if a % 2 == 0:
+                pn = ps_n.tile([P, 2, OUT], F32)
+                pn_t[s, a // 2] = pn
+            for g in range(2):
+                s0 = (g * STEPS[s] + a) * P
+                nc.tensor.matmul_mx(
+                    out=pn_t[s, a // 2][:, a % 2, :],
+                    lhsT=codes_t[s][:, s0 : s0 + P].bitcast(FP8X4),
+                    lhsT_scale=scl_t[s][:, s0 : s0 + P],
+                    rhs=w_codes[g][:].bitcast(FP8X4),
+                    rhs_scale=w_scl[g][:],
+                    start=(g == 0),
+                    stop=(g == 1),
+                )
 
         def bias_add(s):
-            g = group_of[s]
-            gn = gsize(g)
-            nb = STEPS[s]
-            n0 = first[s] - first[GROUPS[g][0]]
-            if s == GROUPS[g][0]:
-                o = opool.tile([P, GMAX * OUT], F32)
-                o_t[g] = o
-            o = o_t[g]
-            pn = pn_t[s]
-            nc.vector.tensor_tensor(
-                out=o[:, 0 : gn * P].rearrange("p (n c) -> p n c", c=P)[:, n0 : n0 + nb],
-                in0=pn[:, 0:nb, 0:P],
-                in1=bb[:, 0:P].unsqueeze(1).to_broadcast([P, nb, P]),
-                op=ALU.add,
-            )
-            nc.vector.tensor_tensor(
-                out=o[:, gn * P : gn * OUT].rearrange("p (s n c) -> p n s c", s=2, c=64)[:, n0 : n0 + nb],
-                in0=pn[:, 0:nb, P:OUT].rearrange("p n (s c) -> p n s c", s=2),
-                in1=bb[:, P:OUT].rearrange("p (s c) -> p s c", s=2).unsqueeze(1).to_broadcast([P, nb, 2, 64]),
-                op=ALU.add,
-            )
-
-        def halves(s):
-            g = group_of[s]
-            gn = gsize(g)
-            nb = STEPS[s]
-            n0 = first[s] - first[GROUPS[g][0]]
-            out = []
-            for lo, t0, nh in ((2 * n0, 0, 2), (2 * gn + n0, 2 * nb, 1)):
-                blocks = o_t[g][:, lo * 64 : (lo + nh * nb) * 64]
-                out.append((blocks.rearrange("p (n h d) -> p n h d", h=nh, d=64)[:, :, :, 0:32], t0, nh))
-            return out
+            n = STEPS[s]
+            o = opool.tile([P, SMAX * OUT], F32)
+            o_t[s] = o
+            for n0 in range(0, n, 2):
+                nb = min(2, n - n0)
+                pn = pn_t[s, n0 // 2]
+                nc.vector.tensor_tensor(
+                    out=o[:, 0 : n * P].rearrange("p (n c) -> p n c", c=P)[:, n0 : n0 + nb],
+                    in0=pn[:, 0:nb, 0:P],
+                    in1=bb[:, 0:P].unsqueeze(1).to_broadcast([P, nb, P]),
+                    op=ALU.add,
+                )
+                nc.vector.tensor_tensor(
+                    out=o[:, n * P : n * OUT].rearrange("p (s n c) -> p n s c", s=2, c=64)[:, n0 : n0 + nb],
+                    in0=pn[:, 0:nb, P:OUT].rearrange("p n (s c) -> p n s c", s=2),
+                    in1=bb[:, P:OUT].rearrange("p (s c) -> p s c", s=2).unsqueeze(1).to_broadcast([P, nb, 2, 64]),
+                    op=ALU.add,
+                )
 
         def rope_mul(s):
-            nb = STEPS[s]
+            n = STEPS[s]
             i0 = first[s]
             t1 = spool.tile([P, 3 * SMAX * 32], F32)
             t2 = spool.tile([P, 3 * SMAX * 32], F32)
             t1_t[s] = t1
             t2_t[s] = t2
-            cv = cos_i[:, i0 * 32 : (i0 + nb) * 32].rearrange("p (n c) -> p n c", c=32)
-            sv = sin_i[:, i0 * 32 : (i0 + nb) * 32].rearrange("p (n j e) -> p n j e", j=16, e=2)
-            for xv, t0, nh in halves(s):
-                tv = t1[:, t0 * 32 : (t0 + nh * nb) * 32].rearrange("p (n h c) -> p n h c", h=nh, c=32)
-                nc.vector.tensor_tensor(out=tv, in0=xv, in1=cv.unsqueeze(2).to_broadcast([P, nb, nh, 32]), op=ALU.mult)
-            for xv, t0, nh in halves(s):
-                tv = t2[:, t0 * 32 : (t0 + nh * nb) * 32].rearrange("p (n h j e) -> p n h j e", h=nh, j=16, e=2)
-                xs = xv.rearrange("p n h (j e) -> p n h j e", e=2)[:, :, :, :, ::-1]
+            cv = cos_i[:, i0 * 32 : (i0 + n) * 32].rearrange("p (n c) -> p n c", c=32)
+            sv = sin_i[:, i0 * 32 : (i0 + n) * 32].rearrange("p (n j e) -> p n j e", j=16, e=2)
+            heads = ((0, 2), (2 * n, 1))
+            for lo, nh in heads:
+                hi = lo + nh * n
+                xv = o_t[s][:, lo * 64 : hi * 64].rearrange("p (n h d) -> p n h d", h=nh, d=64)[:, :, :, 0:32]
+                tv = t1[:, lo * 32 : hi * 32].rearrange("p (n h c) -> p n h c", h=nh, c=32)
+                nc.vector.tensor_tensor(out=tv, in0=xv, in1=cv.unsqueeze(2).to_broadcast([P, n, nh, 32]), op=ALU.mult)
+            for lo, nh in heads:
+                hi = lo + nh * n
+                xv = o_t[s][:, lo * 64 : hi * 64].rearrange("p (n h j e) -> p n h j e", h=nh, j=32, e=2)
+                xs = xv[:, :, :, 0:16, ::-1]
+                tv = t2[:, lo * 32 : hi * 32].rearrange("p (n h j e) -> p n h j e", h=nh, j=16, e=2)
                 for h in range(nh):
                     nc.vector.tensor_tensor(out=tv[:, :, h], in0=xs[:, :, h], in1=sv, op=ALU.mult)
 
         def rope_add(s):
-            nb = STEPS[s]
-            for xv, t0, nh in halves(s):
-                lo, hi = t0 * 32, (t0 + nh * nb) * 32
-                nc.gpsimd.tensor_tensor(
-                    out=xv,
-                    in0=t1_t[s][:, lo:hi].rearrange("p (n h c) -> p n h c", h=nh, c=32),
-                    in1=t2_t[s][:, lo:hi].rearrange("p (n h c) -> p n h c", h=nh, c=32),
-                    op=ALU.add,
-                )
+            n = STEPS[s]
+            engine = nc.vector if s >= ns - 3 else nc.gpsimd
+            engine.tensor_tensor(
+                out=o_t[s][:, 0 : n * 192].rearrange("p (b d) -> p b d", d=64)[:, :, 0:32],
+                in0=t1_t[s][:, 0 : n * 96].rearrange("p (b c) -> p b c", c=32),
+                in1=t2_t[s][:, 0 : n * 96].rearrange("p (b c) -> p b c", c=32),
+                op=ALU.add,
+            )
 
-        def store(g):
-            gn = gsize(g)
-            i0 = first[GROUPS[g][0]]
-            o = o_t[g]
-            nc.sync.dma_start(out=q_v[:, i0 : i0 + gn, :], in_=o[:, 0 : gn * P].rearrange("p (n c) -> p n c", c=P))
-            nc.sync.dma_start(
-                out=k_v[:, i0 : i0 + gn, :], in_=o[:, gn * P : gn * 192].rearrange("p (n c) -> p n c", c=64)
-            )
-            nc.sync.dma_start(
-                out=v_v[:, i0 : i0 + gn, :], in_=o[:, gn * 192 : gn * OUT].rearrange("p (n c) -> p n c", c=64)
-            )
+        def store(s):
+            n = STEPS[s]
+            i0 = first[s]
+            o = o_t[s]
+            for view, lo, w in ((q_v, 0, P), (k_v, P, 64), (v_v, 192, 64)):
+                nc.sync.dma_start(
+                    out=view[:, i0 : i0 + n, :],
+                    in_=o[:, n * lo : n * (lo + w)].rearrange("p (n c) -> p n c", c=w),
+                )
 
         ident = const.tile([P, P], F32)
         make_identity(nc, ident[:])
@@ -226,8 +194,8 @@ def tile_selfattention_pa_t_kernel(tc, hidden_states, cos, sin, W_qkv, b_qkv, ou
         cos_i = const.tile([P, NT * 32], BF16)
         sin_i = const.tile([P, NT * 32], BF16)
 
-        def tables(g):
-            lo, hi = first[GROUPS[g][0]] * 32, (first[GROUPS[g][0]] + gsize(g)) * 32
+        def tables(s):
+            lo, hi = first[s] * 32, (first[s] + STEPS[s]) * 32
             for dst, src in ((cos_i, cos_sb), (sin_i, sin_sb)):
                 nc.scalar.copy(
                     out=dst[:, lo:hi].rearrange("p (i j e) -> p i j e", j=16, e=2),
@@ -256,30 +224,31 @@ def tile_selfattention_pa_t_kernel(tc, hidden_states, cos, sin, W_qkv, b_qkv, ou
                 w_codes.append(wc)
                 w_scl.append(ws)
 
-        loaded = XB
-        for s in range(-2, ns + 3):
+        for s in range(-2, ns + 2):
+            for a in range(0, SMAX, 2):
+                if 0 <= s + 2 < ns:
+                    for b in range(a, min(a + 2, STEPS[s + 2])):
+                        transp(s + 2, b)
+                        copyout(s + 2, b)
+                if 0 <= s < ns:
+                    for b in range(a, min(a + 2, STEPS[s])):
+                        mx(s, b)
             if 0 <= s + 2 < ns:
-                transp(s + 2)
-                copyout(s + 2)
-                c, ca = chunk_of[first[s + 2] + STEPS[s + 2] - 1]
-                if ca == LOADS[c] - 1 and loaded < len(LOADS):
-                    load(loaded)
-                    loaded += 1
-                    if loaded == 8:
-                        load_tables(20, NT)
+                if s + 2 + XB < ns:
+                    load(s + 2 + XB)
+                if s + 2 == 2:
+                    load_tables(20, NT)
             if s == -2:
                 bias_prep()
                 w_prep()
-            if 0 <= s < ns and s == GROUPS[group_of[s]][-1 if s < 3 else 0]:
-                tables(group_of[s])
-            if 0 <= s - 3 < ns:
-                rope_mul(s - 3)
-                rope_add(s - 3)
-                if s - 3 == GROUPS[group_of[s - 3]][-1]:
-                    store(group_of[s - 3])
+            if 0 <= s - 1 < ns and s >= 2:
+                for r in (0, 1) if s == 2 else (s - 1,):
+                    tables(r)
             if 0 <= s + 1 < ns:
                 quant(s + 1)
-            if 0 <= s < ns:
-                mx(s)
+            if 0 <= s - 2 < ns:
+                rope_mul(s - 2)
+                rope_add(s - 2)
+                store(s - 2)
             if 0 <= s - 1 < ns:
                 bias_add(s - 1)

@@ -16,7 +16,7 @@ T, H, OUT = 8192, 1024, 256
 NT = T // P
 FLOPS = 2 * T * H * OUT
 
-STEPS = [1, 1, 2, 2, 2] + [4] * 13 + [2, 1, 1]
+STEPS = [1, 1] + [2] * 5 + [4] * 12 + [2, 2]
 XB = 6
 SMAX = 4
 
@@ -130,23 +130,22 @@ def tile_selfattention_pa_t_kernel(tc, hidden_states, cos, sin, W_qkv, b_qkv, ou
                 xv = o_t[s][:, lo * 64 : hi * 64].rearrange("p (n h d) -> p n h d", h=nh, d=64)[:, :, :, 0:32]
                 tv = t1[:, lo * 32 : hi * 32].rearrange("p (n h c) -> p n h c", h=nh, c=32)
                 nc.vector.tensor_tensor(out=tv, in0=xv, in1=cv.unsqueeze(2).to_broadcast([P, n, nh, 32]), op=ALU.mult)
-            for lo, nh in heads:
-                hi = lo + nh * n
-                xv = o_t[s][:, lo * 64 : hi * 64].rearrange("p (n h j e) -> p n h j e", h=nh, j=32, e=2)
-                xs = xv[:, :, :, 0:16, ::-1]
+                xs = xv.rearrange("p n h (j e) -> p n h j e", e=2)[:, :, :, :, ::-1]
                 tv = t2[:, lo * 32 : hi * 32].rearrange("p (n h j e) -> p n h j e", h=nh, j=16, e=2)
-                for h in range(nh):
-                    nc.vector.tensor_tensor(out=tv[:, :, h], in0=xs[:, :, h], in1=sv, op=ALU.mult)
+                nc.vector.tensor_tensor(
+                    out=tv, in0=xs, in1=sv.unsqueeze(2).to_broadcast([P, n, nh, 16, 2]), op=ALU.mult
+                )
 
         def rope_add(s):
             n = STEPS[s]
-            engine = nc.vector if s >= ns - 3 else nc.gpsimd
-            engine.tensor_tensor(
-                out=o_t[s][:, 0 : n * 192].rearrange("p (b d) -> p b d", d=64)[:, :, 0:32],
-                in0=t1_t[s][:, 0 : n * 96].rearrange("p (b c) -> p b c", c=32),
-                in1=t2_t[s][:, 0 : n * 96].rearrange("p (b c) -> p b c", c=32),
-                op=ALU.add,
-            )
+            engine = nc.vector if s >= ns - 2 else nc.gpsimd
+            for lo, hi in ((0, 2 * n), (2 * n, 3 * n)):
+                engine.tensor_tensor(
+                    out=o_t[s][:, lo * 64 : hi * 64].rearrange("p (b d) -> p b d", d=64)[:, :, 0:32],
+                    in0=t1_t[s][:, lo * 32 : hi * 32].rearrange("p (b c) -> p b c", c=32),
+                    in1=t2_t[s][:, lo * 32 : hi * 32].rearrange("p (b c) -> p b c", c=32),
+                    op=ALU.add,
+                )
 
         def store(s):
             n = STEPS[s]
@@ -167,13 +166,17 @@ def tile_selfattention_pa_t_kernel(tc, hidden_states, cos, sin, W_qkv, b_qkv, ou
         warm = const.tile([P, 1], F32)
         nc.scalar.copy(out=warm[:], in_=ones[:, 0:1])
 
+        w_raw = const.tile([P, 2 * 4 * OUT], BF16)
+        w_view = W_qkv.rearrange("(g p t) c -> g p (t c)", g=2, t=4)
+
+        def load_w(g):
+            nc.sync.dma_start(out=w_raw[:, g * 1024 : (g + 1) * 1024], in_=w_view[g])
+
         load(0)
         nc.sync.dma_start(out=b_row[0:1, :], in_=b_qkv.rearrange("(o c) -> o c", o=1))
-        w_raw = const.tile([P, 2 * 4 * OUT], BF16)
-        nc.sync.dma_start(
-            out=w_raw[:].rearrange("p (g f) -> p g f", g=2),
-            in_=W_qkv.rearrange("(g p t) c -> p g (t c)", g=2, t=4),
-        )
+        load(1)
+        load_w(0)
+        load_w(1)
         sin_sb = const.tile([P, NT * 32], BF16)
         cos_sb = const.tile([P, NT * 32], BF16)
 
@@ -186,10 +189,10 @@ def tile_selfattention_pa_t_kernel(tc, hidden_states, cos, sin, W_qkv, b_qkv, ou
             sneg = sin_sb[:, lo * 32 : hi * 32].rearrange("p (i e j) -> p i e j", e=2, j=16)[:, :, 0, :]
             nc.gpsimd.tensor_scalar(out=sneg, in0=sneg, scalar1=-1.0, scalar2=0.0, op0=ALU.mult, op1=ALU.add)
 
-        for c in range(1, 5):
+        load(2)
+        load_tables(0, 12)
+        for c in range(3, XB):
             load(c)
-        load_tables(0, 20)
-        load(5)
 
         cos_i = const.tile([P, NT * 32], BF16)
         sin_i = const.tile([P, NT * 32], BF16)
@@ -212,15 +215,18 @@ def tile_selfattention_pa_t_kernel(tc, hidden_states, cos, sin, W_qkv, b_qkv, ou
         w_codes, w_scl = [], []
 
         def w_prep():
+            w_grp = []
             for g in range(2):
-                w_grp = const.tile([P, OUT * 4], BF16, name="w_grp%d" % g, align_bytes=64)
+                wg = const.tile([P, OUT * 4], BF16, name="w_grp%d" % g, align_bytes=64)
                 nc.vector.tensor_copy(
-                    out=w_grp[:].rearrange("p (c t) -> p c t", t=4),
+                    out=wg[:].rearrange("p (c t) -> p c t", t=4),
                     in_=w_raw[:, g * 1024 : (g + 1) * 1024].rearrange("p (t c) -> p c t", t=4),
                 )
+                w_grp.append(wg)
+            for g in range(2):
                 wc = const.tile([P, OUT], U32, name="w_codes%d" % g, align_bytes=64)
                 ws = const.tile([P, OUT], U8, name="w_scl%d" % g, align_bytes=64)
-                nc.vector.quantize_mx(out=wc[:].bitcast(FP8X4), scales=ws[:], in_=w_grp[:])
+                nc.vector.quantize_mx(out=wc[:].bitcast(FP8X4), scales=ws[:], in_=w_grp[g][:])
                 w_codes.append(wc)
                 w_scl.append(ws)
 
@@ -237,13 +243,12 @@ def tile_selfattention_pa_t_kernel(tc, hidden_states, cos, sin, W_qkv, b_qkv, ou
                 if s + 2 + XB < ns:
                     load(s + 2 + XB)
                 if s + 2 == 2:
-                    load_tables(20, NT)
+                    load_tables(12, NT)
             if s == -2:
                 bias_prep()
                 w_prep()
-            if 0 <= s - 1 < ns and s >= 2:
-                for r in (0, 1) if s == 2 else (s - 1,):
-                    tables(r)
+            if 0 <= s - 1 < ns:
+                tables(s - 1)
             if 0 <= s + 1 < ns:
                 quant(s + 1)
             if 0 <= s - 2 < ns:

@@ -16,7 +16,7 @@ T, H, OUT = 8192, 1024, 256
 NT = T // P
 FLOPS = 2 * T * H * OUT
 
-STEPS = [1, 1] + [2] * 5 + [4] * 12 + [2, 2]
+STEPS = [1, 1] + [2] * 3 + [4] * 13 + [2, 2]
 XB = 6
 SMAX = 4
 
@@ -80,40 +80,40 @@ def tile_selfattention_pa_t_kernel(tc, hidden_states, cos, sin, W_qkv, b_qkv, ou
             scl_t[s] = scl
 
         def mx(s, a):
-            if a % 2 == 0:
-                pn = ps_n.tile([P, 2, OUT], F32)
-                pn_t[s, a // 2] = pn
-            for g in range(2):
-                s0 = (g * STEPS[s] + a) * P
-                nc.tensor.matmul_mx(
-                    out=pn_t[s, a // 2][:, a % 2, :],
-                    lhsT=codes_t[s][:, s0 : s0 + P].bitcast(FP8X4),
-                    lhsT_scale=scl_t[s][:, s0 : s0 + P],
-                    rhs=w_codes[g][:].bitcast(FP8X4),
-                    rhs_scale=w_scl[g][:],
-                    start=(g == 0),
-                    stop=(g == 1),
-                )
+            if a == 0:
+                pq = ps_n.tile([P, SMAX, P], F32, tag="pn")
+                pkv = ps_n.tile([P, SMAX, P], F32, tag="pn")
+                pn_t[s] = (pq, pkv)
+            for c in range(2):
+                for g in range(2):
+                    s0 = (g * STEPS[s] + a) * P
+                    nc.tensor.matmul_mx(
+                        out=pn_t[s][c][:, a, :],
+                        lhsT=codes_t[s][:, s0 : s0 + P].bitcast(FP8X4),
+                        lhsT_scale=scl_t[s][:, s0 : s0 + P],
+                        rhs=w_codes[g][:, c * P : (c + 1) * P].bitcast(FP8X4),
+                        rhs_scale=w_scl[g][:, c * P : (c + 1) * P],
+                        start=(g == 0),
+                        stop=(g == 1),
+                    )
 
         def bias_add(s):
             n = STEPS[s]
             o = opool.tile([P, SMAX * OUT], F32)
             o_t[s] = o
-            for n0 in range(0, n, 2):
-                nb = min(2, n - n0)
-                pn = pn_t[s, n0 // 2]
-                nc.vector.tensor_tensor(
-                    out=o[:, 0 : n * P].rearrange("p (n c) -> p n c", c=P)[:, n0 : n0 + nb],
-                    in0=pn[:, 0:nb, 0:P],
-                    in1=bb[:, 0:P].unsqueeze(1).to_broadcast([P, nb, P]),
-                    op=ALU.add,
-                )
-                nc.vector.tensor_tensor(
-                    out=o[:, n * P : n * OUT].rearrange("p (s n c) -> p n s c", s=2, c=64)[:, n0 : n0 + nb],
-                    in0=pn[:, 0:nb, P:OUT].rearrange("p n (s c) -> p n s c", s=2),
-                    in1=bb[:, P:OUT].rearrange("p (s c) -> p s c", s=2).unsqueeze(1).to_broadcast([P, nb, 2, 64]),
-                    op=ALU.add,
-                )
+            pq, pkv = pn_t[s]
+            nc.vector.tensor_tensor(
+                out=o[:, 0 : n * P].rearrange("p (n c) -> p n c", c=P),
+                in0=pq[:, 0:n, :],
+                in1=bb[:, 0:P].unsqueeze(1).to_broadcast([P, n, P]),
+                op=ALU.add,
+            )
+            nc.vector.tensor_tensor(
+                out=o[:, n * P : n * OUT].rearrange("p (s n c) -> p n s c", s=2, c=64),
+                in0=pkv[:, 0:n, :].rearrange("p n (s c) -> p n s c", s=2),
+                in1=bb[:, P:OUT].rearrange("p (s c) -> p s c", s=2).unsqueeze(1).to_broadcast([P, n, 2, 64]),
+                op=ALU.add,
+            )
 
         def rope_mul(s):
             n = STEPS[s]
@@ -186,11 +186,13 @@ def tile_selfattention_pa_t_kernel(tc, hidden_states, cos, sin, W_qkv, b_qkv, ou
                     out=dst[:, lo * 32 : hi * 32].rearrange("p (i c) -> p i c", c=32),
                     in_=src.rearrange("(p i) c -> p i c", i=NT)[:, lo:hi, :],
                 )
+
+        def negate(lo, hi):
             sneg = sin_sb[:, lo * 32 : hi * 32].rearrange("p (i e j) -> p i e j", e=2, j=16)[:, :, 0, :]
-            nc.gpsimd.tensor_scalar(out=sneg, in0=sneg, scalar1=-1.0, scalar2=0.0, op0=ALU.mult, op1=ALU.add)
+            nc.scalar.activation(out=sneg, in_=sneg, func=ACT.Copy, scale=-1.0)
 
         load(2)
-        load_tables(0, 12)
+        load_tables(0, 8)
         for c in range(3, XB):
             load(c)
 
@@ -243,11 +245,15 @@ def tile_selfattention_pa_t_kernel(tc, hidden_states, cos, sin, W_qkv, b_qkv, ou
                 if s + 2 + XB < ns:
                     load(s + 2 + XB)
                 if s + 2 == 2:
-                    load_tables(12, NT)
+                    load_tables(8, NT)
             if s == -2:
                 bias_prep()
                 w_prep()
             if 0 <= s - 1 < ns:
+                if s - 1 == 0:
+                    negate(0, 8)
+                if first[s - 1] == 8:
+                    negate(8, NT)
                 tables(s - 1)
             if 0 <= s + 1 < ns:
                 quant(s + 1)

from contextlib import ExitStack

import concourse.mybir as mybir
from concourse.masks import make_identity

F32 = mybir.dt.float32
BF16 = mybir.dt.bfloat16
U32 = mybir.dt.uint32
U8 = mybir.dt.uint8
FP8X4 = mybir.dt.float8_e4m3fn_x4
ALU = mybir.AluOpType
ACT = mybir.ActivationFunctionType

P = 128
T, H, OUT = 8192, 1024, 256
NT = T // P
FLOPS = 2 * T * H * OUT

STEPS = [1, 1] + [2] * 3 + [4] * 13 + [2, 2]
XB = 6
SMAX = 4


def tile_selfattention_pa_t_kernel(tc, hidden_states, cos, sin, W_qkv, b_qkv, out_0, out_1, out_2):
    nc = tc.nc
    ns = len(STEPS)
    first = [sum(STEPS[:s]) for s in range(ns)]
    x_v = hidden_states.rearrange("(p i) k -> p i k", i=NT)
    q_v = out_0.rearrange("(p i) h d -> p i (h d)", i=NT)
    k_v = out_1.rearrange("(p i) h d -> p i (h d)", i=NT)
    v_v = out_2.rearrange("(p i) h d -> p i (h d)", i=NT)

    with ExitStack() as ctx:
        ctx.enter_context(tc.manual_schedule())
        const = ctx.enter_context(tc.tile_pool(name="const", bufs=1))
        xpool = ctx.enter_context(tc.tile_pool(name="xpool", bufs=XB))
        gpool = ctx.enter_context(tc.tile_pool(name="gpool", bufs=4))
        opool = ctx.enter_context(tc.tile_pool(name="opool", bufs=8))
        spool = ctx.enter_context(tc.tile_pool(name="spool", bufs=4))
        ps_x = ctx.enter_context(tc.psum_pool(name="ps_x", bufs=4))
        ps_n = ctx.enter_context(tc.psum_pool(name="ps_n", bufs=4))

        x_t, xt_t, grp_t, codes_t, scl_t, pn_t, o_t, t1_t, t2_t = {}, {}, {}, {}, {}, {}, {}, {}, {}

        def load(s):
            n = STEPS[s]
            xc = xpool.tile([P, SMAX * H], BF16)
            nc.sync.dma_start(
                out=xc[:, 0 : n * H].rearrange("p (n k) -> p n k", k=H),
                in_=x_v[:, first[s] : first[s] + n, :],
            )
            x_t[s] = xc

        def transp(s, a):
            xw = x_t[s][:].bitcast(F32)
            xt = ps_x.tile([P, 4, P], F32)
            for b in range(4):
                w0 = a * 512 + (b // 2) * 256 + b % 2
                nc.tensor.transpose(xt[:, b, :], xw[:, w0 : w0 + 255 : 2], ident[:])
            xt_t[s, a] = xt

        def copyout(s, a):
            n = STEPS[s]
            if a == 0:
                grp = gpool.tile([P, SMAX * H], BF16, align_bytes=64)
                grp_t[s] = grp
            gw = grp_t[s][:].bitcast(F32)[:, 0 : n * 512].rearrange("p (g a m u) -> p g a m u", g=2, a=n, u=2)
            nc.scalar.copy(out=gw[:, :, a], in_=xt_t[s, a][:].rearrange("p (g u) m -> p g m u", u=2))

        def quant(s):
            n = STEPS[s]
            codes = gpool.tile([P, SMAX * 256], U32, align_bytes=64)
            scl = gpool.tile([P, SMAX * 256], U8, align_bytes=64)
            nc.vector.quantize_mx(
                out=codes[:, 0 : n * 256].bitcast(FP8X4),
                scales=scl[:, 0 : n * 256],
                in_=grp_t[s][:, 0 : n * H],
            )
            codes_t[s] = codes
            scl_t[s] = scl

        def mx(s, a):
            if a == 0:
                pq = ps_n.tile([P, SMAX, P], F32, tag="pn")
                pkv = ps_n.tile([P, SMAX, P], F32, tag="pn")
                pn_t[s] = (pq, pkv)
            for c in range(2):
                for g in range(2):
                    s0 = (g * STEPS[s] + a) * P
                    nc.tensor.matmul_mx(
                        out=pn_t[s][c][:, a, :],
                        lhsT=codes_t[s][:, s0 : s0 + P].bitcast(FP8X4),
                        lhsT_scale=scl_t[s][:, s0 : s0 + P],
                        rhs=w_codes[g][:, c * P : (c + 1) * P].bitcast(FP8X4),
                        rhs_scale=w_scl[g][:, c * P : (c + 1) * P],
                        start=(g == 0),
                        stop=(g == 1),
                    )

        def bias_add(s):
            n = STEPS[s]
            o = opool.tile([P, SMAX * OUT], F32)
            o_t[s] = o
            pq, pkv = pn_t[s]
            nc.vector.tensor_tensor(
                out=o[:, 0 : n * P].rearrange("p (n c) -> p n c", c=P),
                in0=pq[:, 0:n, :],
                in1=bb[:, 0:P].unsqueeze(1).to_broadcast([P, n, P]),
                op=ALU.add,
            )
            nc.vector.tensor_tensor(
                out=o[:, n * P : n * OUT].rearrange("p (s n c) -> p n s c", s=2, c=64),
                in0=pkv[:, 0:n, :].rearrange("p n (s c) -> p n s c", s=2),
                in1=bb[:, P:OUT].rearrange("p (s c) -> p s c", s=2).unsqueeze(1).to_broadcast([P, n, 2, 64]),
                op=ALU.add,
            )

        def rope_mul(s):
            n = STEPS[s]
            i0 = first[s]
            t1 = spool.tile([P, 3 * SMAX * 32], F32)
            t2 = spool.tile([P, 3 * SMAX * 32], F32)
            t1_t[s] = t1
            t2_t[s] = t2
            cv = cos_i[:, i0 * 32 : (i0 + n) * 32].rearrange("p (n c) -> p n c", c=32)
            sv = sin_i[:, i0 * 32 : (i0 + n) * 32].rearrange("p (n j e) -> p n j e", j=16, e=2)
            heads = ((0, 2), (2 * n, 1))
            for lo, nh in heads:
                hi = lo + nh * n
                xv = o_t[s][:, lo * 64 : hi * 64].rearrange("p (n h d) -> p n h d", h=nh, d=64)[:, :, :, 0:32]
                tv = t1[:, lo * 32 : hi * 32].rearrange("p (n h c) -> p n h c", h=nh, c=32)
                nc.vector.tensor_tensor(out=tv, in0=xv, in1=cv.unsqueeze(2).to_broadcast([P, n, nh, 32]), op=ALU.mult)
                xs = xv.rearrange("p n h (j e) -> p n h j e", e=2)[:, :, :, :, ::-1]
                tv = t2[:, lo * 32 : hi * 32].rearrange("p (n h j e) -> p n h j e", h=nh, j=16, e=2)
                nc.vector.tensor_tensor(
                    out=tv, in0=xs, in1=sv.unsqueeze(2).to_broadcast([P, n, nh, 16, 2]), op=ALU.mult
                )

        def rope_add(s):
            n = STEPS[s]
            engine = nc.vector if s >= ns - 2 else nc.gpsimd
            for lo, hi in ((0, 2 * n), (2 * n, 3 * n)):
                engine.tensor_tensor(
                    out=o_t[s][:, lo * 64 : hi * 64].rearrange("p (b d) -> p b d", d=64)[:, :, 0:32],
                    in0=t1_t[s][:, lo * 32 : hi * 32].rearrange("p (b c) -> p b c", c=32),
                    in1=t2_t[s][:, lo * 32 : hi * 32].rearrange("p (b c) -> p b c", c=32),
                    op=ALU.add,
                )

        def store(s):
            n = STEPS[s]
            i0 = first[s]
            o = o_t[s]
            for view, lo, w in ((q_v, 0, P), (k_v, P, 64), (v_v, 192, 64)):
                nc.sync.dma_start(
                    out=view[:, i0 : i0 + n, :],
                    in_=o[:, n * lo : n * (lo + w)].rearrange("p (n c) -> p n c", c=w),
                )

        ident = const.tile([P, P], F32)
        make_identity(nc, ident[:])
        b_row = const.tile([P, OUT], BF16)
        nc.vector.memset(b_row[:], 0.0)
        ones = const.tile([P, P], BF16)
        nc.vector.memset(ones[:], 1.0)
        warm = const.tile([P, 1], F32)
        nc.scalar.copy(out=warm[:], in_=ones[:, 0:1])

        w_raw = const.tile([P, 2 * 4 * OUT], BF16)
        w_view = W_qkv.rearrange("(g p t) c -> g p (t c)", g=2, t=4)

        def load_w(g):
            nc.sync.dma_start(out=w_raw[:, g * 1024 : (g + 1) * 1024], in_=w_view[g])

        load(0)
        nc.sync.dma_start(out=b_row[0:1, :], in_=b_qkv.rearrange("(o c) -> o c", o=1))
        load(1)
        load_w(0)
        load_w(1)
        sin_sb = const.tile([P, NT * 32], BF16)
        cos_sb = const.tile([P, NT * 32], BF16)

        def load_tables(lo, hi):
            for dst, src in ((sin_sb, sin), (cos_sb, cos)):
                nc.sync.dma_start(
                    out=dst[:, lo * 32 : hi * 32].rearrange("p (i c) -> p i c", c=32),
                    in_=src.rearrange("(p i) c -> p i c", i=NT)[:, lo:hi, :],
                )

        def negate(lo, hi):
            sneg = sin_sb[:, lo * 32 : hi * 32].rearrange("p (i e j) -> p i e j", e=2, j=16)[:, :, 0, :]
            nc.scalar.activation(out=sneg, in_=sneg, func=ACT.Copy, scale=-1.0)

        load(2)
        load_tables(0, 8)
        for c in range(3, XB):
            load(c)

        cos_i = const.tile([P, NT * 32], BF16)
        sin_i = const.tile([P, NT * 32], BF16)

        def tables(s):
            lo, hi = first[s] * 32, (first[s] + STEPS[s]) * 32
            for dst, src in ((cos_i, cos_sb), (sin_i, sin_sb)):
                nc.scalar.copy(
                    out=dst[:, lo:hi].rearrange("p (i j e) -> p i j e", j=16, e=2),
                    in_=src[:, lo:hi].rearrange("p (i e j) -> p i j e", e=2, j=16),
                )

        bb = const.tile([P, OUT], F32)

        def bias_prep():
            pbias = ps_n.tile([P, 2, OUT], F32, tag="pn")
            nc.tensor.matmul(out=pbias[:, 0, :], lhsT=ones[:], rhs=b_row[:], start=True, stop=True)
            nc.scalar.copy(out=bb[:], in_=pbias[:, 0, :])

        w_codes, w_scl = [], []

        def w_prep():
            w_grp = []
            for g in range(2):
                wg = const.tile([P, OUT * 4], BF16, name="w_grp%d" % g, align_bytes=64)
                nc.vector.tensor_copy(
                    out=wg[:].rearrange("p (c t) -> p c t", t=4),
                    in_=w_raw[:, g * 1024 : (g + 1) * 1024].rearrange("p (t c) -> p c t", t=4),
                )
                w_grp.append(wg)
            for g in range(2):
                wc = const.tile([P, OUT], U32, name="w_codes%d" % g, align_bytes=64)
                ws = const.tile([P, OUT], U8, name="w_scl%d" % g, align_bytes=64)
                nc.vector.quantize_mx(out=wc[:].bitcast(FP8X4), scales=ws[:], in_=w_grp[g][:])
                w_codes.append(wc)
                w_scl.append(ws)

        for s in range(-2, ns + 2):
            for a in range(0, SMAX, 2):
                if 0 <= s + 2 < ns:
                    for b in range(a, min(a + 2, STEPS[s + 2])):
                        transp(s + 2, b)
                        copyout(s + 2, b)
                if 0 <= s < ns:
                    for b in range(a, min(a + 2, STEPS[s])):
                        mx(s, b)
            if 0 <= s + 2 < ns:
                if s + 2 + XB < ns:
                    load(s + 2 + XB)
                if s + 2 == 2:
                    load_tables(8, NT)
            if s == -2:
                bias_prep()
                w_prep()
            if 0 <= s - 1 < ns:
                if s - 1 == 0:
                    negate(0, 8)
                if first[s - 1] == 8:
                    negate(8, NT)
                tables(s - 1)
            if 0 <= s + 1 < ns:
                quant(s + 1)
            if 0 <= s - 2 < ns:
                rope_mul(s - 2)
                rope_add(s - 2)
                store(s - 2)
            if 0 <= s - 1 < ns:
                bias_add(s - 1)
